import numpy as np
import ml_dtypes


def mxq(x, axis, fmt="e4m3"):
    dtype, down = {"e4m3": (ml_dtypes.float8_e4m3fn, 7), "e5m2": (ml_dtypes.float8_e5m2, 14)}[fmt]
    v = np.moveaxis(np.asarray(x, np.float32).astype(ml_dtypes.bfloat16).astype(np.float64), axis, -1)
    blocks = v.reshape(v.shape[:-1] + (-1, 32))
    amax = np.abs(blocks).max(-1, keepdims=True)
    byte = np.maximum(np.where(amax > 0, np.frexp(amax)[1] - 1 + 127, 0) - down, 1)
    scale = np.exp2(byte - 127.0)
    codes = (blocks / scale).astype(np.float32).astype(dtype).astype(np.float64)
    return np.moveaxis((codes * scale).reshape(v.shape), -1, axis)


WIDE = False


def mx_kscale(k):
    if not WIDE:
        return np.ones(k)
    levels = np.array([10, -10, 5, -5, 0])
    a = np.random.permutation(np.resize(levels, k // 512 * 4)).reshape(k // 512, 4)
    idx = np.arange(k)
    return np.exp2(a[idx // 512, idx % 128 // 32])


BF16 = ml_dtypes.bfloat16


def bf(x):
    return np.asarray(x, np.float32).astype(BF16)


def f64(x):
    return np.asarray(x).astype(np.float64)


E2M1 = np.array([0.0, 0.5, 1.0, 1.5, 2.0, 3.0, 4.0, 6.0, -0.0, -0.5, -1.0, -1.5, -2.0, -3.0, -4.0, -6.0])


def pack_weight(w, fmt):
    k, n = w.shape
    w = f64(bf(w)).reshape(k // 32, 32, n)
    amax = np.abs(w).max(1)
    if fmt == "e4m3":
        byte = np.frexp(amax)[1] - 1 + 127 - 7
    else:
        mant, ex = np.frexp(amax / 6.0)
        byte = np.where(mant > 0.5, ex, ex - 1) + 127
    byte = np.clip(np.where(amax > 0, byte, 1), 1, 254)
    scaled = (w * np.exp2(127.0 - byte)[:, None, :]).reshape(k, n).astype(np.float32)
    by_word = np.ascontiguousarray(scaled.reshape(k // 512, 128, 4, n).transpose(0, 1, 3, 2))
    if fmt == "e4m3":
        words = by_word.astype(ml_dtypes.float8_e4m3fn).view(np.uint8)
    else:
        c = by_word.astype(ml_dtypes.float4_e2m1fn).view(np.uint8) & 0xF
        words = c[..., 0::2] | (c[..., 1::2] << 4)
    return np.ascontiguousarray(words), np.ascontiguousarray(byte.astype(np.uint8).reshape(k // 512, 16, n))


def unpack_weight(words, scales, fmt):
    g, p, n, _ = words.shape
    if fmt == "e4m3":
        vals = np.ascontiguousarray(words).view(ml_dtypes.float8_e4m3fn).astype(np.float64)
    else:
        nib = np.empty((g, p, n, 4), np.uint8)
        nib[..., 0::2] = words & 0xF
        nib[..., 1::2] = words >> 4
        vals = E2M1[nib]
    vals = vals * np.repeat(np.exp2(scales.astype(np.float64) - 127.0), 8, axis=1)[..., None]
    return vals.transpose(0, 1, 3, 2).reshape(g * 512, n)


B, H = 512, 1024
EPS = 1e-5
FMT = "e4m3"


def layernorm(x, gamma, beta):
    mu = np.mean(x, axis=-1, keepdims=True)
    var = np.var(x, axis=-1, keepdims=True)
    return (x - mu) / np.sqrt(var + EPS) * gamma + beta


def sigmoid(v):
    return 1.0 / (1.0 + np.exp(-v))


def setup_inputs():
    s = mx_kscale(H)
    inp = bf(np.random.standard_normal((B, H)) * s)
    hx = bf(np.random.standard_normal((B, H)))
    W_words, W_scales = pack_weight(np.random.standard_normal((H, 3 * H)) / np.sqrt(H) / s[:, None], FMT)
    U_words, U_scales = pack_weight(np.random.standard_normal((H, 3 * H)) / np.sqrt(H), FMT)
    return {"input": inp,
            "hx": hx,
            "W_words": W_words,
            "W_scales": W_scales,
            "U_words": U_words,
            "U_scales": U_scales,
            "b": bf(np.random.standard_normal(3 * H) * 0.1),
            "W_gamma": bf(1.0 + np.random.standard_normal(3 * H) * 0.1),
            "W_beta": bf(np.random.standard_normal(3 * H) * 0.1),
            "U_gamma": bf(1.0 + np.random.standard_normal(3 * H) * 0.1),
            "U_beta": bf(np.random.standard_normal(3 * H) * 0.1)}


def reference(input, hx, W_words, W_scales, U_words, U_scales, b, W_gamma, W_beta, U_gamma, U_beta):
    hx = f64(hx)
    b = f64(b)
    xw = layernorm(mxq(f64(input), 1, "e4m3") @ unpack_weight(W_words, W_scales, FMT), f64(W_gamma), f64(W_beta))
    hu = layernorm(mxq(hx, 1, "e4m3") @ unpack_weight(U_words, U_scales, FMT), f64(U_gamma), f64(U_beta))
    xw0, xw1, xw2 = xw[:, :H], xw[:, H:2 * H], xw[:, 2 * H:]
    hu0, hu1, hu2 = hu[:, :H], hu[:, H:2 * H], hu[:, 2 * H:]
    b0, b1, b2 = b[:H], b[H:2 * H], b[2 * H:]
    z = sigmoid(xw0 + hu0 + b0)
    r = sigmoid(xw1 + hu1 + b1)
    hx_ = np.tanh(r * hu2 + xw2 + b2)
    return (1.0 - z) * hx_ + z * hx

@@ -1,0 +1,338 @@
+from contextlib import ExitStack
+
+import concourse.mybir as mybir
+from concourse.masks import make_identity
+
+F32 = mybir.dt.float32
+BF16 = mybir.dt.bfloat16
+I32 = mybir.dt.int32
+U32 = mybir.dt.uint32
+U8 = mybir.dt.uint8
+FP8X4 = mybir.dt.float8_e4m3fn_x4
+ALU = mybir.AluOpType
+FUNC = mybir.ActivationFunctionType
+
+P = 128
+PACK = 4
+BATCH = 512
+HIDDEN = 1024
+GATES = 3
+WIDE = GATES * HIDDEN
+EPS = 1e-5
+
+M_TILES = BATCH // P
+K_PASSES = HIDDEN // (P * PACK)
+BANK = 512
+CHUNKS = WIDE // BANK
+J_TILES = HIDDEN // P
+J_PER_CHUNK = BANK // P
+N_TILES = WIDE // P
+STATS = 6
+HX_AFTER_CHUNK = 3
+
+FLOPS = 2 * 2 * BATCH * HIDDEN * WIDE
+
+
+def tile_lngrucell_kernel(
+    tc, x_in, hx, W_words, W_scales, U_words, U_scales, b, W_gamma, W_beta, U_gamma, U_beta, out
+):
+    nc = tc.nc
+    with ExitStack() as ctx:
+        keep = ctx.enter_context(tc.tile_pool(name="keep", bufs=1))
+        stage = ctx.enter_context(tc.tile_pool(name="stage", bufs=3))
+        work = ctx.enter_context(tc.tile_pool(name="work", bufs=3))
+        psum = ctx.enter_context(tc.psum_pool(name="psum", bufs=8))
+        ctx.enter_context(tc.manual_schedule())
+
+        def bank():
+            return psum.tile([P, BANK], F32, name="bank", tag="bank")
+
+        identity = keep.tile([P, P], F32, name="identity")
+        make_identity(nc, identity[:])
+
+        one = keep.tile([P, 1], F32, name="one")
+        nc.vector.memset(one[:], 1.0)
+        warmed = keep.tile([P, 1], F32, name="warmed")
+
+        def load_table_of(func):
+            nc.scalar.activation(out=warmed[:], in_=one[:], func=func)
+
+        load_table_of(FUNC.Sqrt)
+
+        planes = keep.tile([P, WIDE], U8, name="planes", align_bytes=64)
+        nc.vector.memset(planes[:].bitcast(I32), 0)
+
+        def make_side(label, x_dram, words_dram, scales_dram, first_plane):
+            return {
+                "x_dram": x_dram,
+                "words_dram": words_dram.rearrange("g p n t -> p g (n t)").bitcast(I32),
+                "scales_dram": scales_dram.bitcast(I32),
+                "plane_row": PACK * first_plane,
+                "x_sb": keep.tile([P, M_TILES, HIDDEN], BF16, name="x_" + label),
+                "w_sb": keep.tile([P, K_PASSES, WIDE], U32, name="w_" + label, align_bytes=64),
+                "codes": keep.tile([P, M_TILES, K_PASSES * P], U32, name="codes_" + label, align_bytes=64),
+                "x_scales": keep.tile([P, M_TILES, K_PASSES * P], U8, name="xs_" + label, align_bytes=64),
+                "rows": keep.tile([P, M_TILES, J_TILES, GATES, P], F32, name="rows_" + label),
+                "stats": keep.tile([P, M_TILES, CHUNKS, STATS], F32, name="stats_" + label),
+                "mean_var": keep.tile([P, M_TILES, 2], F32, name="mv_" + label),
+                "var_eps": keep.tile([P, M_TILES], F32, name="ve_" + label),
+                "std": keep.tile([P, M_TILES], F32, name="std_" + label),
+                "rstd": keep.tile([P, M_TILES], F32, name="rstd_" + label),
+                "neg_mean": keep.tile([P, M_TILES], F32, name="nm_" + label),
+            }
+
+        x_side = make_side("x", x_in, W_words, W_scales, 0)
+        h_side = make_side("h", hx, U_words, U_scales, K_PASSES)
+
+        def load_x(side):
+            tiles = side["x_dram"].rearrange("(m p) k -> m p k", p=P)
+            for m in range(M_TILES):
+                nc.sync.dma_start(out=side["x_sb"][:, m, :], in_=tiles[m])
+
+        def load_scales(side):
+            for quadrant in range(4):
+                first = 32 * quadrant + side["plane_row"]
+                nc.sync.dma_start(
+                    out=planes[first : first + PACK * K_PASSES, :].bitcast(I32),
+                    in_=side["scales_dram"][:, PACK * quadrant : PACK * (quadrant + 1), :],
+                )
+
+        def load_words(side, c):
+            cols = slice(c * BANK, (c + 1) * BANK)
+            nc.sync.dma_start(out=side["w_sb"][:, :, cols].bitcast(I32), in_=side["words_dram"][:, :, cols])
+
+        for side in (x_side, h_side):
+            load_x(side)
+            load_scales(side)
+            for c in range(CHUNKS):
+                load_words(side, c)
+
+        vectors = (W_gamma, U_gamma, W_beta, U_beta, b)
+        vec_rows = keep.tile([P, P], BF16, name="vec_rows")
+        nc.vector.memset(vec_rows[:].bitcast(I32), 0)
+        for v in range(len(vectors)):
+            nc.gpsimd.dma_start(
+                out=vec_rows[v * N_TILES : (v + 1) * N_TILES, :],
+                in_=vectors[v].rearrange("(t p) -> t p", p=P),
+            )
+        vec_rows_f32 = keep.tile([P, P], F32, name="vec_rows_f32")
+        vec_cols = keep.tile([P, P], F32, name="vec_cols")
+        gamma_w = vec_cols[:, 0 * N_TILES : 1 * N_TILES]
+        gamma_u = vec_cols[:, 1 * N_TILES : 2 * N_TILES]
+        beta_w = vec_cols[:, 2 * N_TILES : 3 * N_TILES]
+        beta_u = vec_cols[:, 3 * N_TILES : 4 * N_TILES]
+        bias_b = vec_cols[:, 4 * N_TILES : 5 * N_TILES]
+        shift = keep.tile([P, N_TILES], F32, name="shift")
+
+        def turn_vectors():
+            nc.vector.tensor_copy(out=vec_rows_f32[:], in_=vec_rows[:])
+            vec_bank = bank()
+            nc.tensor.transpose(out=vec_bank[:, :P], in_=vec_rows_f32[:], identity=identity[:])
+            nc.vector.tensor_copy(out=vec_cols[:], in_=vec_bank[:, :P])
+            nc.vector.tensor_add(out=shift[:], in0=beta_w, in1=bias_b)
+            sigmoid_tiles = 2 * J_TILES
+            nc.vector.tensor_add(
+                out=shift[:, :sigmoid_tiles], in0=shift[:, :sigmoid_tiles], in1=beta_u[:, :sigmoid_tiles]
+            )
+
+        def column(table, t):
+            return table[:, t : t + 1]
+
+        def quantise_x(side):
+            for m in range(M_TILES):
+                words = side["x_sb"][:, m, :].bitcast(F32)
+                turned = bank()
+                for g in range(K_PASSES):
+                    for u in range(2):
+                        piece = 2 * g + u
+                        nc.tensor.transpose(
+                            out=turned[:, piece * P : (piece + 1) * P],
+                            in_=words[:, 2 * P * g + u : 2 * P * (g + 1) : 2],
+                            identity=identity[:],
+                        )
+                grouped = stage.tile([P, K_PASSES * P * PACK], BF16, name="grouped", align_bytes=64)
+                nc.scalar.copy(
+                    out=grouped[:].bitcast(F32).rearrange("p (g r u) -> p g r u", g=K_PASSES, u=2),
+                    in_=turned[:].rearrange("p (g u r) -> p g r u", g=K_PASSES, u=2),
+                )
+                nc.vector.quantize_mx(
+                    out=side["codes"][:, m, :].bitcast(FP8X4),
+                    scales=side["x_scales"][:, m, :],
+                    in_=grouped[:],
+                )
+
+        def multiply_chunk(side, c):
+            gate = c // (CHUNKS // GATES)
+            j_first = J_PER_CHUNK * (c % (CHUNKS // GATES))
+            cols = slice(c * BANK, (c + 1) * BANK)
+            for m in range(M_TILES):
+                acc = bank()
+                for g in range(K_PASSES):
+                    batch_rows = slice(g * P, (g + 1) * P)
+                    nc.tensor.matmul_mx(
+                        out=acc[:],
+                        lhsT=side["codes"][:, m, batch_rows].bitcast(FP8X4),
+                        lhsT_scale=side["x_scales"][:, m, batch_rows],
+                        rhs=side["w_sb"][:, g, cols].bitcast(FP8X4),
+                        rhs_scale=planes[side["plane_row"] + PACK * g : P, cols],
+                        start=(g == 0),
+                        stop=(g == K_PASSES - 1),
+                    )
+                landed = side["rows"][:, m, j_first : j_first + J_PER_CHUNK, gate, :]
+                nc.scalar.copy(out=landed, in_=acc[:].rearrange("p (j n) -> p j n", n=P))
+                nc.vector.bn_stats(out=side["stats"][:, m, c, :], in_=landed)
+
+        def row_moments(side):
+            for m in range(M_TILES):
+                nc.vector.bn_aggr(
+                    out=side["mean_var"][:, m, :],
+                    in_=side["stats"][:, m, :, :].rearrange("p c s -> p (c s)"),
+                )
+            nc.vector.tensor_scalar_add(out=side["var_eps"][:], in0=side["mean_var"][:, :, 1], scalar1=EPS)
+
+        def row_factors(side):
+            nc.scalar.activation(out=side["std"][:], in_=side["var_eps"][:], func=FUNC.Sqrt)
+            nc.vector.reciprocal(out=side["rstd"][:], in_=side["std"][:])
+            nc.vector.tensor_scalar_mul(out=side["neg_mean"][:], in0=side["mean_var"][:, :, 0], scalar1=-1.0)
+
+        def normalise(side, j_first, j_count):
+            for m in range(M_TILES):
+                run = side["rows"][:, m, j_first : j_first + j_count, :, :].rearrange("p j g n -> p (j g n)")
+                nc.gpsimd.tensor_scalar(
+                    out=run,
+                    in0=run,
+                    scalar1=side["neg_mean"][:, m : m + 1],
+                    scalar2=side["rstd"][:, m : m + 1],
+                    op0=ALU.add,
+                    op1=ALU.mult,
+                )
+
+        quantise_x(x_side)
+        for c in range(CHUNKS):
+            multiply_chunk(x_side, c)
+            if c == HX_AFTER_CHUNK:
+                quantise_x(h_side)
+                turn_vectors()
+        row_moments(x_side)
+        for c in range(CHUNKS):
+            multiply_chunk(h_side, c)
+            if c == 0:
+                row_factors(x_side)
+                normalise(x_side, 0, J_TILES)
+
+        RESET, UPDATE, CAND = 1, 0, 2
+        live = {}
+
+        def turn(side, gate, j):
+            turned = bank()
+            for m in range(M_TILES):
+                nc.tensor.transpose(
+                    out=turned[:, m * P : (m + 1) * P],
+                    in_=side["rows"][:, m, j, gate, :],
+                    identity=identity[:],
+                )
+            return turned
+
+        def start_sigmoid_gates(j):
+            for gate in (RESET, UPDATE):
+                t = gate * J_TILES + j
+                value = work.tile([P, BATCH], F32, name="gate%d" % gate)
+                nc.scalar.activation(
+                    out=value[:], in_=turn(x_side, gate, j)[:], func=FUNC.Identity,
+                    scale=column(gamma_w, t), bias=column(shift, t),
+                )
+                live[gate, j] = value
+
+        def turn_h(j):
+            for gate in (CAND, RESET, UPDATE):
+                live["h", gate, j] = turn(h_side, gate, j)
+
+        def start_candidate(j):
+            t = CAND * J_TILES + j
+            cand = work.tile([P, BATCH], F32, name="cand")
+            nc.scalar.activation(
+                out=cand[:], in_=live["h", CAND, j][:], func=FUNC.Identity,
+                scale=column(gamma_u, t), bias=column(beta_u, t),
+            )
+            live[CAND, j] = cand
+
+        def finish_sigmoid_gate(gate, j):
+            value = live[gate, j]
+            nc.vector.scalar_tensor_tensor(
+                out=value[:], in0=live["h", gate, j][:], scalar=column(gamma_u, gate * J_TILES + j), in1=value[:],
+                op0=ALU.mult, op1=ALU.add,
+            )
+            nc.scalar.activation(out=value[:], in_=value[:], func=FUNC.Sigmoid)
+
+        def apply_reset(j):
+            nc.vector.tensor_mul(out=live[CAND, j][:], in0=live[CAND, j][:], in1=live[RESET, j][:])
+
+        def finish_candidate(j):
+            t = CAND * J_TILES + j
+            cand = live[CAND, j]
+            nc.vector.scalar_tensor_tensor(
+                out=cand[:], in0=turn(x_side, CAND, j)[:], scalar=column(gamma_w, t), in1=cand[:],
+                op0=ALU.mult, op1=ALU.add,
+            )
+            nc.scalar.activation(out=cand[:], in_=cand[:], func=FUNC.Tanh, bias=column(shift, t))
+
+        out_tiles = out.rearrange("(m p) n -> p m n", p=P)
+
+        def turn_back(j):
+            for gate in (CAND, UPDATE):
+                turned = bank()
+                for m in range(M_TILES):
+                    nc.tensor.transpose(
+                        out=turned[:, m * P : (m + 1) * P],
+                        in_=live[gate, j][:, m * P : (m + 1) * P],
+                        identity=identity[:],
+                    )
+                live["rows", gate, j] = turned[:].rearrange("p (m n) -> p m n", n=P)
+
+        def blend_subtract(j):
+            diff = work.tile([P, M_TILES, P], F32, name="diff")
+            nc.vector.tensor_sub(
+                out=diff[:], in0=h_side["x_sb"][:, :, j * P : (j + 1) * P], in1=live["rows", CAND, j]
+            )
+            live["diff", j] = diff
+
+        def blend_scale(j):
+            nc.vector.tensor_mul(out=live["diff", j][:], in0=live["diff", j][:], in1=live["rows", UPDATE, j])
+
+        def blend_add_and_store(j):
+            result = work.tile([P, M_TILES, P], F32, name="result")
+            nc.vector.tensor_add(out=result[:], in0=live["diff", j][:], in1=live["rows", CAND, j])
+            nc.sync.dma_start(out=out_tiles[:, :, j * P : (j + 1) * P], in_=result[:])
+
+        start_sigmoid_gates(0)
+        row_moments(h_side)
+        row_factors(h_side)
+        load_table_of(FUNC.Sigmoid)
+        for j in range(J_TILES):
+            normalise(h_side, j, 1)
+        turn_h(0)
+
+        for j in range(J_TILES + 1):
+            gates_now = j < J_TILES
+            blend_now = j >= 1
+            turn_next = j + 1 < J_TILES
+            if blend_now:
+                turn_back(j - 1)
+            if gates_now:
+                start_candidate(j)
+                finish_sigmoid_gate(RESET, j)
+                finish_sigmoid_gate(UPDATE, j)
+            if blend_now:
+                blend_subtract(j - 1)
+            if turn_next:
+                start_sigmoid_gates(j + 1)
+            if gates_now:
+                apply_reset(j)
+            if blend_now:
+                blend_scale(j - 1)
+            if gates_now:
+                finish_candidate(j)
+            if blend_now:
+                blend_add_and_store(j - 1)
+            if turn_next:
+                turn_h(j + 1)

@@ -29,6 +29,8 @@ J_PER_CHUNK = BANK // P
 N_TILES = WIDE // P
 STATS = 6
 HX_AFTER_CHUNK = 3
+X_LOADS = 2
+X_LEAD = 2
 
 FLOPS = 2 * 2 * BATCH * HIDDEN * WIDE
 
@@ -59,15 +61,12 @@ def tile_lngrucell_kernel(
 
         load_table_of(FUNC.Sqrt)
 
-        planes = keep.tile([P, WIDE], U8, name="planes", align_bytes=64)
-        nc.vector.memset(planes[:].bitcast(I32), 0)
-
-        def make_side(label, x_dram, words_dram, scales_dram, first_plane):
+        def make_side(label, x_dram, words_dram, scales_dram):
             return {
                 "x_dram": x_dram,
                 "words_dram": words_dram.rearrange("g p n t -> p g (n t)").bitcast(I32),
                 "scales_dram": scales_dram.bitcast(I32),
-                "plane_row": PACK * first_plane,
+                "planes": keep.tile([P, WIDE], U8, name="planes_" + label, align_bytes=64),
                 "x_sb": keep.tile([P, M_TILES, HIDDEN], BF16, name="x_" + label),
                 "w_sb": keep.tile([P, K_PASSES, WIDE], U32, name="w_" + label, align_bytes=64),
                 "codes": keep.tile([P, M_TILES, K_PASSES * P], U32, name="codes_" + label, align_bytes=64),
@@ -79,21 +78,25 @@ def tile_lngrucell_kernel(
                 "std": keep.tile([P, M_TILES], F32, name="std_" + label),
                 "rstd": keep.tile([P, M_TILES], F32, name="rstd_" + label),
                 "neg_mean": keep.tile([P, M_TILES], F32, name="nm_" + label),
+                "neg_mean_rstd": keep.tile([P, M_TILES], F32, name="nmr_" + label),
             }
 
-        x_side = make_side("x", x_in, W_words, W_scales, 0)
-        h_side = make_side("h", hx, U_words, U_scales, K_PASSES)
+        x_side = make_side("x", x_in, W_words, W_scales)
+        h_side = make_side("h", hx, U_words, U_scales)
+        for side in (x_side, h_side):
+            nc.vector.memset(side["planes"][:].bitcast(I32), 0)
 
         def load_x(side):
-            tiles = side["x_dram"].rearrange("(m p) k -> m p k", p=P)
-            for m in range(M_TILES):
-                nc.sync.dma_start(out=side["x_sb"][:, m, :], in_=tiles[m])
+            halves = side["x_dram"].rearrange("(l m p) k -> l p m k", l=X_LOADS, p=P)
+            per_load = M_TILES // X_LOADS
+            for l in range(X_LOADS):
+                nc.sync.dma_start(out=side["x_sb"][:, l * per_load : (l + 1) * per_load, :], in_=halves[l])
 
         def load_scales(side):
             for quadrant in range(4):
-                first = 32 * quadrant + side["plane_row"]
+                first = 32 * quadrant
                 nc.sync.dma_start(
-                    out=planes[first : first + PACK * K_PASSES, :].bitcast(I32),
+                    out=side["planes"][first : first + PACK * K_PASSES, :].bitcast(I32),
                     in_=side["scales_dram"][:, PACK * quadrant : PACK * (quadrant + 1), :],
                 )
 
@@ -125,7 +128,6 @@ def tile_lngrucell_kernel(
         shift = keep.tile([P, N_TILES], F32, name="shift")
 
         def turn_vectors():
-            nc.vector.tensor_copy(out=vec_rows_f32[:], in_=vec_rows[:])
             vec_bank = bank()
             nc.tensor.transpose(out=vec_bank[:, :P], in_=vec_rows_f32[:], identity=identity[:])
             nc.vector.tensor_copy(out=vec_cols[:], in_=vec_bank[:, :P])
@@ -174,51 +176,56 @@ def tile_lngrucell_kernel(
                         lhsT=side["codes"][:, m, batch_rows].bitcast(FP8X4),
                         lhsT_scale=side["x_scales"][:, m, batch_rows],
                         rhs=side["w_sb"][:, g, cols].bitcast(FP8X4),
-                        rhs_scale=planes[side["plane_row"] + PACK * g : P, cols],
+                        rhs_scale=side["planes"][PACK * g : P, cols],
                         start=(g == 0),
                         stop=(g == K_PASSES - 1),
                     )
                 landed = side["rows"][:, m, j_first : j_first + J_PER_CHUNK, gate, :]
                 nc.scalar.copy(out=landed, in_=acc[:].rearrange("p (j n) -> p j n", n=P))
                 nc.vector.bn_stats(out=side["stats"][:, m, c, :], in_=landed)
-
-        def row_moments(side):
-            for m in range(M_TILES):
-                nc.vector.bn_aggr(
-                    out=side["mean_var"][:, m, :],
-                    in_=side["stats"][:, m, :, :].rearrange("p c s -> p (c s)"),
-                )
-            nc.vector.tensor_scalar_add(out=side["var_eps"][:], in0=side["mean_var"][:, :, 1], scalar1=EPS)
+                if c == CHUNKS - 1:
+                    nc.vector.bn_aggr(
+                        out=side["mean_var"][:, m, :],
+                        in_=side["stats"][:, m, :, :].rearrange("p c s -> p (c s)"),
+                    )
+            if c == CHUNKS - 1:
+                nc.vector.tensor_scalar_add(out=side["var_eps"][:], in0=side["mean_var"][:, :, 1], scalar1=EPS)
 
         def row_factors(side):
             nc.scalar.activation(out=side["std"][:], in_=side["var_eps"][:], func=FUNC.Sqrt)
             nc.vector.reciprocal(out=side["rstd"][:], in_=side["std"][:])
             nc.vector.tensor_scalar_mul(out=side["neg_mean"][:], in0=side["mean_var"][:, :, 0], scalar1=-1.0)
+            nc.vector.tensor_mul(out=side["neg_mean_rstd"][:], in0=side["neg_mean"][:], in1=side["rstd"][:])
 
-        def normalise(side, j_first, j_count):
-            for m in range(M_TILES):
-                run = side["rows"][:, m, j_first : j_first + j_count, :, :].rearrange("p j g n -> p (j g n)")
-                nc.gpsimd.tensor_scalar(
-                    out=run,
-                    in0=run,
-                    scalar1=side["neg_mean"][:, m : m + 1],
-                    scalar2=side["rstd"][:, m : m + 1],
-                    op0=ALU.add,
-                    op1=ALU.mult,
-                )
+        def normalise(engine, side, j, m):
+            run = side["rows"][:, m, j, :, :].rearrange("p g n -> p (g n)")
+            engine.tensor_scalar(
+                out=run, in0=run,
+                scalar1=side["neg_mean"][:, m : m + 1], scalar2=side["rstd"][:, m : m + 1],
+                op0=ALU.add, op1=ALU.mult,
+            )
+
+        def normalise_on_scalar(side, j, m):
+            run = side["rows"][:, m, j, :, :].rearrange("p g n -> p (g n)")
+            nc.scalar.activation(
+                out=run, in_=run, func=FUNC.Identity,
+                scale=side["rstd"][:, m : m + 1], bias=side["neg_mean_rstd"][:, m : m + 1],
+            )
 
         quantise_x(x_side)
         for c in range(CHUNKS):
             multiply_chunk(x_side, c)
             if c == HX_AFTER_CHUNK:
-                quantise_x(h_side)
+                nc.vector.tensor_copy(out=vec_rows_f32[:], in_=vec_rows[:])
                 turn_vectors()
-        row_moments(x_side)
+                quantise_x(h_side)
         for c in range(CHUNKS):
             multiply_chunk(h_side, c)
             if c == 0:
                 row_factors(x_side)
-                normalise(x_side, 0, J_TILES)
+                for j in range(J_TILES):
+                    for m in range(M_TILES):
+                        normalise(nc.gpsimd, x_side, j, m)
 
         RESET, UPDATE, CAND = 1, 0, 2
         live = {}
@@ -236,12 +243,18 @@ def tile_lngrucell_kernel(
         def start_sigmoid_gates(j):
             for gate in (RESET, UPDATE):
                 t = gate * J_TILES + j
-                value = work.tile([P, BATCH], F32, name="gate%d" % gate)
+                value = work.tile([P, BATCH], F32, name="gate%d" % gate, bufs=X_LEAD + 2)
                 nc.scalar.activation(
                     out=value[:], in_=turn(x_side, gate, j)[:], func=FUNC.Identity,
                     scale=column(gamma_w, t), bias=column(shift, t),
                 )
                 live[gate, j] = value
+
+        def normalise_h(j, on_vector):
+            for m in range(on_vector):
+                normalise(nc.vector, h_side, j, m)
+            for m in range(on_vector, M_TILES):
+                normalise_on_scalar(h_side, j, m)
 
         def turn_h(j):
             for gate in (CAND, RESET, UPDATE):
@@ -305,11 +318,11 @@ def tile_lngrucell_kernel(
             nc.sync.dma_start(out=out_tiles[:, :, j * P : (j + 1) * P], in_=result[:])
 
         start_sigmoid_gates(0)
-        row_moments(h_side)
         row_factors(h_side)
         load_table_of(FUNC.Sigmoid)
-        for j in range(J_TILES):
-            normalise(h_side, j, 1)
+        normalise_h(0, M_TILES)
+        for j in range(1, X_LEAD):
+            start_sigmoid_gates(j)
         turn_h(0)
 
         for j in range(J_TILES + 1):
@@ -322,10 +335,12 @@ def tile_lngrucell_kernel(
                 start_candidate(j)
                 finish_sigmoid_gate(RESET, j)
                 finish_sigmoid_gate(UPDATE, j)
+            if turn_next:
+                normalise_h(j + 1, M_TILES // 2)
             if blend_now:
                 blend_subtract(j - 1)
-            if turn_next:
-                start_sigmoid_gates(j + 1)
+            if j + X_LEAD < J_TILES:
+                start_sigmoid_gates(j + X_LEAD)
             if gates_now:
                 apply_reset(j)
             if blend_now:

@@ -31,6 +31,7 @@ STATS = 6
 HX_AFTER_CHUNK = 3
 X_LOADS = 2
 X_LEAD = 2
+H_LEAD = 2
 
 FLOPS = 2 * 2 * BATCH * HIDDEN * WIDE
 
@@ -51,6 +52,8 @@ def tile_lngrucell_kernel(
 
         identity = keep.tile([P, P], F32, name="identity")
         make_identity(nc, identity[:])
+        identity_bf16 = keep.tile([P, P], BF16, name="identity_bf16")
+        make_identity(nc, identity_bf16[:])
 
         one = keep.tile([P, 1], F32, name="one")
         nc.vector.memset(one[:], 1.0)
@@ -118,7 +121,6 @@ def tile_lngrucell_kernel(
                 out=vec_rows[v * N_TILES : (v + 1) * N_TILES, :],
                 in_=vectors[v].rearrange("(t p) -> t p", p=P),
             )
-        vec_rows_f32 = keep.tile([P, P], F32, name="vec_rows_f32")
         vec_cols = keep.tile([P, P], F32, name="vec_cols")
         gamma_w = vec_cols[:, 0 * N_TILES : 1 * N_TILES]
         gamma_u = vec_cols[:, 1 * N_TILES : 2 * N_TILES]
@@ -128,9 +130,12 @@ def tile_lngrucell_kernel(
         shift = keep.tile([P, N_TILES], F32, name="shift")
 
         def turn_vectors():
-            vec_bank = bank()
-            nc.tensor.transpose(out=vec_bank[:, :P], in_=vec_rows_f32[:], identity=identity[:])
-            nc.vector.tensor_copy(out=vec_cols[:], in_=vec_bank[:, :P])
+            vec_bank = psum.tile([P, P], BF16, name="vec_bank", tag="bank")
+            nc.tensor.transpose(out=vec_bank[:], in_=vec_rows[:], identity=identity_bf16[:])
+            return vec_bank
+
+        def keep_vectors(vec_bank):
+            nc.vector.tensor_copy(out=vec_cols[:], in_=vec_bank[:])
             nc.vector.tensor_add(out=shift[:], in0=beta_w, in1=bias_b)
             sigmoid_tiles = 2 * J_TILES
             nc.vector.tensor_add(
@@ -216,9 +221,9 @@ def tile_lngrucell_kernel(
         for c in range(CHUNKS):
             multiply_chunk(x_side, c)
             if c == HX_AFTER_CHUNK:
-                nc.vector.tensor_copy(out=vec_rows_f32[:], in_=vec_rows[:])
-                turn_vectors()
+                vec_bank = turn_vectors()
                 quantise_x(h_side)
+                keep_vectors(vec_bank)
         for c in range(CHUNKS):
             multiply_chunk(h_side, c)
             if c == 0:
@@ -280,11 +285,14 @@ def tile_lngrucell_kernel(
         def apply_reset(j):
             nc.vector.tensor_mul(out=live[CAND, j][:], in0=live[CAND, j][:], in1=live[RESET, j][:])
 
+        def turn_x_candidate(j):
+            live["x", CAND, j] = turn(x_side, CAND, j)
+
         def finish_candidate(j):
             t = CAND * J_TILES + j
             cand = live[CAND, j]
             nc.vector.scalar_tensor_tensor(
-                out=cand[:], in0=turn(x_side, CAND, j)[:], scalar=column(gamma_w, t), in1=cand[:],
+                out=cand[:], in0=live["x", CAND, j][:], scalar=column(gamma_w, t), in1=cand[:],
                 op0=ALU.mult, op1=ALU.add,
             )
             nc.scalar.activation(out=cand[:], in_=cand[:], func=FUNC.Tanh, bias=column(shift, t))
@@ -321,6 +329,8 @@ def tile_lngrucell_kernel(
         row_factors(h_side)
         load_table_of(FUNC.Sigmoid)
         normalise_h(0, M_TILES)
+        for j in range(1, H_LEAD):
+            normalise_h(j, M_TILES // 2)
         for j in range(1, X_LEAD):
             start_sigmoid_gates(j)
         turn_h(0)
@@ -329,14 +339,16 @@ def tile_lngrucell_kernel(
             gates_now = j < J_TILES
             blend_now = j >= 1
             turn_next = j + 1 < J_TILES
+            if gates_now:
+                turn_x_candidate(j)
             if blend_now:
                 turn_back(j - 1)
             if gates_now:
                 start_candidate(j)
                 finish_sigmoid_gate(RESET, j)
                 finish_sigmoid_gate(UPDATE, j)
-            if turn_next:
-                normalise_h(j + 1, M_TILES // 2)
+            if j + H_LEAD < J_TILES:
+                normalise_h(j + H_LEAD, M_TILES // 2)
             if blend_now:
                 blend_subtract(j - 1)
             if j + X_LEAD < J_TILES:

@@ -28,10 +28,11 @@ J_TILES = HIDDEN // P
 J_PER_CHUNK = BANK // P
 N_TILES = WIDE // P
 STATS = 6
-HX_AFTER_CHUNK = 3
-X_LOADS = 2
-X_LEAD = 2
-H_LEAD = 2
+BANKS = 8
+W_ARRIVES = 3
+LAST_ON_SCALAR = (0, 2)
+NORM_J = 2
+GATE_TILES = 16
 
 FLOPS = 2 * 2 * BATCH * HIDDEN * WIDE
 
@@ -42,13 +43,19 @@ def tile_lngrucell_kernel(
     nc = tc.nc
     with ExitStack() as ctx:
         keep = ctx.enter_context(tc.tile_pool(name="keep", bufs=1))
-        stage = ctx.enter_context(tc.tile_pool(name="stage", bufs=3))
+        stage = ctx.enter_context(tc.tile_pool(name="stage", bufs=2))
         work = ctx.enter_context(tc.tile_pool(name="work", bufs=3))
-        psum = ctx.enter_context(tc.psum_pool(name="psum", bufs=8))
+        psum = ctx.enter_context(tc.psum_pool(name="psum", bufs=1))
         ctx.enter_context(tc.manual_schedule())
 
-        def bank():
-            return psum.tile([P, BANK], F32, name="bank", tag="bank")
+        def bank(k, width=BANK, dtype=F32):
+            return psum.tile([P, width], dtype, name="bank", tag="bank%d" % k)
+
+        turns = [0]
+
+        def next_bank(width=BANK, dtype=F32):
+            turns[0] += 1
+            return bank((turns[0] - 1) % BANKS, width, dtype)
 
         identity = keep.tile([P, P], F32, name="identity")
         make_identity(nc, identity[:])
@@ -62,11 +69,11 @@ def tile_lngrucell_kernel(
         def load_table_of(func):
             nc.scalar.activation(out=warmed[:], in_=one[:], func=func)
 
-        load_table_of(FUNC.Sqrt)
+        load_table_of(FUNC.Abs_reciprocal_sqrt)
 
         def make_side(label, x_dram, words_dram, scales_dram):
             return {
-                "x_dram": x_dram,
+                "x_dram": x_dram.rearrange("(m p) k -> m p k", p=P),
                 "words_dram": words_dram.rearrange("g p n t -> p g (n t)").bitcast(I32),
                 "scales_dram": scales_dram.bitcast(I32),
                 "planes": keep.tile([P, WIDE], U8, name="planes_" + label, align_bytes=64),
@@ -77,10 +84,8 @@ def tile_lngrucell_kernel(
                 "rows": keep.tile([P, M_TILES, J_TILES, GATES, P], F32, name="rows_" + label),
                 "stats": keep.tile([P, M_TILES, CHUNKS, STATS], F32, name="stats_" + label),
                 "mean_var": keep.tile([P, M_TILES, 2], F32, name="mv_" + label),
-                "var_eps": keep.tile([P, M_TILES], F32, name="ve_" + label),
-                "std": keep.tile([P, M_TILES], F32, name="std_" + label),
-                "rstd": keep.tile([P, M_TILES], F32, name="rstd_" + label),
                 "neg_mean": keep.tile([P, M_TILES], F32, name="nm_" + label),
+                "rstd": keep.tile([P, M_TILES], F32, name="rstd_" + label),
                 "neg_mean_rstd": keep.tile([P, M_TILES], F32, name="nmr_" + label),
             }
 
@@ -89,11 +94,8 @@ def tile_lngrucell_kernel(
         for side in (x_side, h_side):
             nc.vector.memset(side["planes"][:].bitcast(I32), 0)
 
-        def load_x(side):
-            halves = side["x_dram"].rearrange("(l m p) k -> l p m k", l=X_LOADS, p=P)
-            per_load = M_TILES // X_LOADS
-            for l in range(X_LOADS):
-                nc.sync.dma_start(out=side["x_sb"][:, l * per_load : (l + 1) * per_load, :], in_=halves[l])
+        def load_x(side, m):
+            nc.sync.dma_start(out=side["x_sb"][:, m, :], in_=side["x_dram"][m])
 
         def load_scales(side):
             for quadrant in range(4):
@@ -107,20 +109,30 @@ def tile_lngrucell_kernel(
             cols = slice(c * BANK, (c + 1) * BANK)
             nc.sync.dma_start(out=side["w_sb"][:, :, cols].bitcast(I32), in_=side["words_dram"][:, :, cols])
 
-        for side in (x_side, h_side):
-            load_x(side)
-            load_scales(side)
-            for c in range(CHUNKS):
-                load_words(side, c)
-
         vectors = (W_gamma, U_gamma, W_beta, U_beta, b)
         vec_rows = keep.tile([P, P], BF16, name="vec_rows")
         nc.vector.memset(vec_rows[:].bitcast(I32), 0)
-        for v in range(len(vectors)):
-            nc.gpsimd.dma_start(
-                out=vec_rows[v * N_TILES : (v + 1) * N_TILES, :],
-                in_=vectors[v].rearrange("(t p) -> t p", p=P),
-            )
+
+        def load_vectors():
+            for v in range(len(vectors)):
+                nc.gpsimd.dma_start(
+                    out=vec_rows[v * N_TILES : (v + 1) * N_TILES, :],
+                    in_=vectors[v].rearrange("(t p) -> t p", p=P),
+                )
+
+        for m in range(M_TILES):
+            load_x(x_side, m)
+        load_scales(x_side)
+        load_vectors()
+        for c in range(CHUNKS):
+            load_words(x_side, c)
+            if c == W_ARRIVES - 1:
+                for m in range(M_TILES):
+                    load_x(h_side, m)
+        load_scales(h_side)
+        for c in range(CHUNKS):
+            load_words(h_side, c)
+
         vec_cols = keep.tile([P, P], F32, name="vec_cols")
         gamma_w = vec_cols[:, 0 * N_TILES : 1 * N_TILES]
         gamma_u = vec_cols[:, 1 * N_TILES : 2 * N_TILES]
@@ -130,7 +142,7 @@ def tile_lngrucell_kernel(
         shift = keep.tile([P, N_TILES], F32, name="shift")
 
         def turn_vectors():
-            vec_bank = psum.tile([P, P], BF16, name="vec_bank", tag="bank")
+            vec_bank = next_bank(P, BF16)
             nc.tensor.transpose(out=vec_bank[:], in_=vec_rows[:], identity=identity_bf16[:])
             return vec_bank
 
@@ -145,98 +157,79 @@ def tile_lngrucell_kernel(
         def column(table, t):
             return table[:, t : t + 1]
 
-        def quantise_x(side):
-            for m in range(M_TILES):
-                words = side["x_sb"][:, m, :].bitcast(F32)
-                turned = bank()
-                for g in range(K_PASSES):
-                    for u in range(2):
-                        piece = 2 * g + u
-                        nc.tensor.transpose(
-                            out=turned[:, piece * P : (piece + 1) * P],
-                            in_=words[:, 2 * P * g + u : 2 * P * (g + 1) : 2],
-                            identity=identity[:],
-                        )
-                grouped = stage.tile([P, K_PASSES * P * PACK], BF16, name="grouped", align_bytes=64)
-                nc.scalar.copy(
-                    out=grouped[:].bitcast(F32).rearrange("p (g r u) -> p g r u", g=K_PASSES, u=2),
-                    in_=turned[:].rearrange("p (g u r) -> p g r u", g=K_PASSES, u=2),
-                )
-                nc.vector.quantize_mx(
-                    out=side["codes"][:, m, :].bitcast(FP8X4),
-                    scales=side["x_scales"][:, m, :],
-                    in_=grouped[:],
+        grouped = {}
+
+        def turn_k(side, m):
+            words = side["x_sb"][:, m, :].bitcast(F32)
+            turned = next_bank()
+            for g in range(K_PASSES):
+                for u in range(2):
+                    piece = 2 * g + u
+                    nc.tensor.transpose(
+                        out=turned[:, piece * P : (piece + 1) * P],
+                        in_=words[:, 2 * P * g + u : 2 * P * (g + 1) : 2],
+                        identity=identity[:],
+                    )
+            copied = stage.tile([P, K_PASSES * P * PACK], BF16, name="copied", align_bytes=64)
+            nc.scalar.copy(
+                out=copied[:].bitcast(F32).rearrange("p (g r u) -> p g r u", g=K_PASSES, u=2),
+                in_=turned[:].rearrange("p (g u r) -> p g r u", g=K_PASSES, u=2),
+            )
+            grouped[m] = copied
+
+        def quantise(side, m):
+            nc.vector.quantize_mx(
+                out=side["codes"][:, m, :].bitcast(FP8X4), scales=side["x_scales"][:, m, :], in_=grouped[m][:]
+            )
+
+        def multiply(side, m, c, acc):
+            cols = slice(c * BANK, (c + 1) * BANK)
+            for g in range(K_PASSES):
+                batch_rows = slice(g * P, (g + 1) * P)
+                nc.tensor.matmul_mx(
+                    out=acc[:],
+                    lhsT=side["codes"][:, m, batch_rows].bitcast(FP8X4),
+                    lhsT_scale=side["x_scales"][:, m, batch_rows],
+                    rhs=side["w_sb"][:, g, cols].bitcast(FP8X4),
+                    rhs_scale=side["planes"][PACK * g : P, cols],
+                    start=(g == 0),
+                    stop=(g == K_PASSES - 1),
                 )
 
-        def multiply_chunk(side, c):
+        def place_of(side, m, c):
             gate = c // (CHUNKS // GATES)
             j_first = J_PER_CHUNK * (c % (CHUNKS // GATES))
-            cols = slice(c * BANK, (c + 1) * BANK)
-            for m in range(M_TILES):
-                acc = bank()
-                for g in range(K_PASSES):
-                    batch_rows = slice(g * P, (g + 1) * P)
-                    nc.tensor.matmul_mx(
-                        out=acc[:],
-                        lhsT=side["codes"][:, m, batch_rows].bitcast(FP8X4),
-                        lhsT_scale=side["x_scales"][:, m, batch_rows],
-                        rhs=side["w_sb"][:, g, cols].bitcast(FP8X4),
-                        rhs_scale=side["planes"][PACK * g : P, cols],
-                        start=(g == 0),
-                        stop=(g == K_PASSES - 1),
-                    )
-                landed = side["rows"][:, m, j_first : j_first + J_PER_CHUNK, gate, :]
-                nc.scalar.copy(out=landed, in_=acc[:].rearrange("p (j n) -> p j n", n=P))
-                nc.vector.bn_stats(out=side["stats"][:, m, c, :], in_=landed)
-                if c == CHUNKS - 1:
-                    nc.vector.bn_aggr(
-                        out=side["mean_var"][:, m, :],
-                        in_=side["stats"][:, m, :, :].rearrange("p c s -> p (c s)"),
-                    )
-            if c == CHUNKS - 1:
-                nc.vector.tensor_scalar_add(out=side["var_eps"][:], in0=side["mean_var"][:, :, 1], scalar1=EPS)
+            return side["rows"][:, m, j_first : j_first + J_PER_CHUNK, gate, :]
 
-        def row_factors(side):
-            nc.scalar.activation(out=side["std"][:], in_=side["var_eps"][:], func=FUNC.Sqrt)
-            nc.vector.reciprocal(out=side["rstd"][:], in_=side["std"][:])
-            nc.vector.tensor_scalar_mul(out=side["neg_mean"][:], in0=side["mean_var"][:, :, 0], scalar1=-1.0)
-            nc.vector.tensor_mul(out=side["neg_mean_rstd"][:], in0=side["neg_mean"][:], in1=side["rstd"][:])
+        def by_tile(acc):
+            return acc[:].rearrange("p (j n) -> p j n", n=P)
 
-        def normalise(engine, side, j, m):
-            run = side["rows"][:, m, j, :, :].rearrange("p g n -> p (g n)")
-            engine.tensor_scalar(
-                out=run, in0=run,
-                scalar1=side["neg_mean"][:, m : m + 1], scalar2=side["rstd"][:, m : m + 1],
-                op0=ALU.add, op1=ALU.mult,
+        def per_row(side, what, m):
+            return side[what][:, m : m + 1]
+
+        def moments(side, m, c, source):
+            nc.vector.bn_stats(out=side["stats"][:, m, c, :], in_=source)
+
+        def mean_and_var(side, m):
+            nc.vector.bn_aggr(
+                out=side["mean_var"][:, m, :], in_=side["stats"][:, m, :, :].rearrange("p c s -> p (c s)")
             )
 
-        def normalise_on_scalar(side, j, m):
-            run = side["rows"][:, m, j, :, :].rearrange("p g n -> p (g n)")
+        def negate_mean(side, tiles):
+            nc.vector.tensor_scalar_mul(
+                out=side["neg_mean"][:, tiles], in0=side["mean_var"][:, tiles, 0], scalar1=-1.0
+            )
+
+        def inverse_std(side, tiles):
             nc.scalar.activation(
-                out=run, in_=run, func=FUNC.Identity,
-                scale=side["rstd"][:, m : m + 1], bias=side["neg_mean_rstd"][:, m : m + 1],
+                out=side["rstd"][:, tiles], in_=side["mean_var"][:, tiles, 1],
+                func=FUNC.Abs_reciprocal_sqrt, bias=EPS,
             )
-
-        quantise_x(x_side)
-        for c in range(CHUNKS):
-            multiply_chunk(x_side, c)
-            if c == HX_AFTER_CHUNK:
-                vec_bank = turn_vectors()
-                quantise_x(h_side)
-                keep_vectors(vec_bank)
-        for c in range(CHUNKS):
-            multiply_chunk(h_side, c)
-            if c == 0:
-                row_factors(x_side)
-                for j in range(J_TILES):
-                    for m in range(M_TILES):
-                        normalise(nc.gpsimd, x_side, j, m)
 
         RESET, UPDATE, CAND = 1, 0, 2
         live = {}
 
-        def turn(side, gate, j):
-            turned = bank()
+        def turn(side, gate, j, turned):
             for m in range(M_TILES):
                 nc.tensor.transpose(
                     out=turned[:, m * P : (m + 1) * P],
@@ -245,121 +238,271 @@ def tile_lngrucell_kernel(
                 )
             return turned
 
-        def start_sigmoid_gates(j):
-            for gate in (RESET, UPDATE):
-                t = gate * J_TILES + j
-                value = work.tile([P, BATCH], F32, name="gate%d" % gate, bufs=X_LEAD + 2)
-                nc.scalar.activation(
-                    out=value[:], in_=turn(x_side, gate, j)[:], func=FUNC.Identity,
-                    scale=column(gamma_w, t), bias=column(shift, t),
+        def scale_and_shift(engine, out, in_, scale, bias):
+            if engine is nc.scalar:
+                nc.scalar.activation(out=out, in_=in_, func=FUNC.Identity, scale=scale, bias=bias)
+            else:
+                nc.vector.tensor_scalar(
+                    out=out, in0=in_, scalar1=scale, scalar2=bias, op0=ALU.mult, op1=ALU.add
                 )
-                live[gate, j] = value
 
-        def normalise_h(j, on_vector):
-            for m in range(on_vector):
-                normalise(nc.vector, h_side, j, m)
-            for m in range(on_vector, M_TILES):
-                normalise_on_scalar(h_side, j, m)
+        def turn_x_gate(gate, j, turned):
+            live["x", gate, j] = turn(x_side, gate, j, turned)
 
-        def turn_h(j):
-            for gate in (CAND, RESET, UPDATE):
-                live["h", gate, j] = turn(h_side, gate, j)
+        def start_gate(engine, gate, j):
+            t = gate * J_TILES + j
+            value = work.tile([P, BATCH], F32, name="gate", bufs=GATE_TILES)
+            scale_and_shift(engine, value[:], live["x", gate, j][:], column(gamma_w, t), column(shift, t))
+            live[gate, j] = value
+
+        def product_x(m, c):
+            acc = next_bank()
+            multiply(x_side, m, c, acc)
+            nc.scalar.copy(out=place_of(x_side, m, c), in_=by_tile(acc))
+            moments(x_side, m, c, place_of(x_side, m, c))
+
+        def normalise_x(m):
+            for j in range(0, J_TILES, NORM_J):
+                run = x_side["rows"][:, m, j : j + NORM_J, :, :].rearrange("p j g n -> p (j g n)")
+                nc.gpsimd.tensor_scalar(
+                    out=run, in0=run,
+                    scalar1=per_row(x_side, "neg_mean", m), scalar2=per_row(x_side, "rstd", m),
+                    op0=ALU.add, op1=ALU.mult,
+                )
+
+        def finish_moments(side, m):
+            mean_and_var(side, m)
+            negate_mean(side, slice(m, m + 1))
+
+        for m in range(M_TILES):
+            turn_k(x_side, m)
+            quantise(x_side, m)
+        for c in range(W_ARRIVES):
+            for m in range(M_TILES):
+                product_x(m, c)
+        vec_bank = turn_vectors()
+        for m in range(M_TILES):
+            turn_k(h_side, m)
+            quantise(h_side, m)
+        keep_vectors(vec_bank)
+        for m in range(M_TILES):
+            for c in range(W_ARRIVES, CHUNKS):
+                product_x(m, c)
+            finish_moments(x_side, m)
+            if m >= 1:
+                inverse_std(x_side, slice(m - 1, m))
+                normalise_x(m - 1)
+
+        h_acc = {}
+        order = (0, 2, 4, 1, 3, 5)
+
+        def product_h(m, k):
+            if m < M_TILES:
+                h_acc[m, k] = bank(k)
+                multiply(h_side, m, order[k], h_acc[m, k])
+                moments(h_side, m, order[k], h_acc[m, k][:])
+
+        def take_out_h(m, k, engine=None):
+            if engine is nc.vector:
+                nc.vector.tensor_scalar(
+                    out=place_of(h_side, m, order[k]), in0=by_tile(h_acc[m, k]),
+                    scalar1=per_row(h_side, "neg_mean", m), scalar2=per_row(h_side, "rstd", m),
+                    op0=ALU.add, op1=ALU.mult,
+                )
+                return
+            nc.scalar.activation(
+                out=place_of(h_side, m, order[k]), in_=by_tile(h_acc[m, k]), func=FUNC.Identity,
+                scale=per_row(h_side, "rstd", m), bias=per_row(h_side, "neg_mean_rstd", m),
+            )
+
+        def row_factors_h(m):
+            tile = slice(m, m + 1)
+            inverse_std(h_side, tile)
+            nc.scalar.activation(
+                out=per_row(h_side, "neg_mean_rstd", m), in_=per_row(h_side, "neg_mean", m), func=FUNC.Copy,
+                scale=per_row(h_side, "rstd", m),
+            )
+
+        ready_gates = [(gate, j) for j in range(J_TILES) for gate in (RESET, UPDATE)]
+        spare = [0]
+        V, S = nc.vector, nc.scalar
+
+        turned_gates = []
+
+        def turn_next_gate(k=None):
+            if ready_gates:
+                gate, j = ready_gates.pop(0)
+                spare[0] += 1
+                turn_x_gate(gate, j, bank(CHUNKS + spare[0] % 2 if k is None else k))
+                turned_gates.append((gate, j))
+
+        def start_next_gate(engine):
+            if turned_gates:
+                start_gate(engine, *turned_gates.pop(0))
+
+        V, S = nc.vector, nc.scalar
+
+        for k in range(CHUNKS):
+            acc = bank(k)
+            multiply(h_side, 0, order[k], acc)
+            nc.scalar.copy(out=place_of(h_side, 0, order[k]), in_=by_tile(acc))
+            moments(h_side, 0, order[k], place_of(h_side, 0, order[k]))
+            if k == 2:
+                inverse_std(x_side, slice(M_TILES - 1, M_TILES))
+                normalise_x(M_TILES - 1)
+        finish_moments(h_side, 0)
+        for k in range(CHUNKS):
+            product_h(1, k)
+        finish_moments(h_side, 1)
+        row_factors_h(0)
+        for j in range(0, J_TILES, NORM_J):
+            run = h_side["rows"][:, 0, j : j + NORM_J, :, :].rearrange("p j g n -> p (j g n)")
+            nc.scalar.activation(
+                out=run, in_=run, func=FUNC.Identity,
+                scale=per_row(h_side, "rstd", 0), bias=per_row(h_side, "neg_mean_rstd", 0),
+            )
+        turn_next_gate()
+        turn_next_gate()
+        for m in range(1, M_TILES - 1):
+            row_factors_h(m)
+            for k in range(CHUNKS):
+                take_out_h(m, k)
+                product_h(m + 1, k)
+            finish_moments(h_side, m + 1)
+            for _ in range(2):
+                start_next_gate(S)
+            for _ in range(2):
+                turn_next_gate()
+            for _ in range(2):
+                start_next_gate(V)
+            for _ in range(2):
+                turn_next_gate()
+        m = M_TILES - 1
+        row_factors_h(m)
+        for k in range(CHUNKS):
+            take_out_h(m, k, S if k in LAST_ON_SCALAR else V)
+        load_table_of(FUNC.Sigmoid)
+
+        def turn_h_gate(gate, j, turned):
+            live["h", gate, j] = turn(h_side, gate, j, turned)
+
+        ALL = slice(0, BATCH)
+        HALVES = (slice(0, BATCH // 2), slice(BATCH // 2, BATCH))
 
         def start_candidate(j):
             t = CAND * J_TILES + j
-            cand = work.tile([P, BATCH], F32, name="cand")
-            nc.scalar.activation(
-                out=cand[:], in_=live["h", CAND, j][:], func=FUNC.Identity,
-                scale=column(gamma_u, t), bias=column(beta_u, t),
-            )
+            cand = work.tile([P, BATCH], F32, name="cand", bufs=4)
+            scale_and_shift(S, cand[:], live["h", CAND, j][:], column(gamma_u, t), column(beta_u, t))
             live[CAND, j] = cand
 
-        def finish_sigmoid_gate(gate, j):
+        def add_h_gate(gate, j):
             value = live[gate, j]
             nc.vector.scalar_tensor_tensor(
                 out=value[:], in0=live["h", gate, j][:], scalar=column(gamma_u, gate * J_TILES + j), in1=value[:],
                 op0=ALU.mult, op1=ALU.add,
             )
-            nc.scalar.activation(out=value[:], in_=value[:], func=FUNC.Sigmoid)
 
-        def apply_reset(j):
-            nc.vector.tensor_mul(out=live[CAND, j][:], in0=live[CAND, j][:], in1=live[RESET, j][:])
+        def sigmoid_gate(gate, j):
+            nc.scalar.activation(out=live[gate, j][:], in_=live[gate, j][:], func=FUNC.Sigmoid)
 
-        def turn_x_candidate(j):
-            live["x", CAND, j] = turn(x_side, CAND, j)
+        def apply_reset(engine, j, part):
+            cand = live[CAND, j][:, part]
+            engine.tensor_tensor(out=cand, in0=cand, in1=live[RESET, j][:, part], op=ALU.mult)
 
-        def finish_candidate(j):
-            t = CAND * J_TILES + j
-            cand = live[CAND, j]
+        def add_x_candidate(j, part):
+            cand = live[CAND, j][:, part]
             nc.vector.scalar_tensor_tensor(
-                out=cand[:], in0=live["x", CAND, j][:], scalar=column(gamma_w, t), in1=cand[:],
+                out=cand, in0=live["x", CAND, j][:, part], scalar=column(gamma_w, CAND * J_TILES + j), in1=cand,
                 op0=ALU.mult, op1=ALU.add,
             )
-            nc.scalar.activation(out=cand[:], in_=cand[:], func=FUNC.Tanh, bias=column(shift, t))
+
+        def finish_candidate(j, part):
+            cand = live[CAND, j][:, part]
+            nc.scalar.activation(out=cand, in_=cand, func=FUNC.Tanh, bias=column(shift, CAND * J_TILES + j))
 
         out_tiles = out.rearrange("(m p) n -> p m n", p=P)
 
-        def turn_back(j):
-            for gate in (CAND, UPDATE):
-                turned = bank()
-                for m in range(M_TILES):
-                    nc.tensor.transpose(
-                        out=turned[:, m * P : (m + 1) * P],
-                        in_=live[gate, j][:, m * P : (m + 1) * P],
-                        identity=identity[:],
-                    )
-                live["rows", gate, j] = turned[:].rearrange("p (m n) -> p m n", n=P)
+        def turn_hx(j, turned):
+            for m in range(M_TILES):
+                nc.tensor.transpose(
+                    out=turned[:, m * P : (m + 1) * P],
+                    in_=h_side["x_sb"][:, m, j * P : (j + 1) * P],
+                    identity=identity_bf16[:],
+                )
+            live["hx", j] = turned
+            live["diff", j] = work.tile([P, BATCH], F32, name="diff")
 
-        def blend_subtract(j):
-            diff = work.tile([P, M_TILES, P], F32, name="diff")
+        def blend_subtract(j, part):
             nc.vector.tensor_sub(
-                out=diff[:], in0=h_side["x_sb"][:, :, j * P : (j + 1) * P], in1=live["rows", CAND, j]
+                out=live["diff", j][:, part], in0=live["hx", j][:, part], in1=live[CAND, j][:, part]
             )
-            live["diff", j] = diff
 
-        def blend_scale(j):
-            nc.vector.tensor_mul(out=live["diff", j][:], in0=live["diff", j][:], in1=live["rows", UPDATE, j])
+        def blend_scale(engine, j, part):
+            diff = live["diff", j][:, part]
+            engine.tensor_tensor(out=diff, in0=diff, in1=live[UPDATE, j][:, part], op=ALU.mult)
 
-        def blend_add_and_store(j):
+        def turn_back(j, turned, part):
+            for m in range(part.start // P, part.stop // P):
+                batch = slice(m * P, (m + 1) * P)
+                for name in (CAND, "diff"):
+                    nc.tensor.matmul(
+                        out=turned[:, batch], lhsT=live[name, j][:, batch], rhs=identity[:],
+                        start=(name == CAND), stop=(name == "diff"), is_transpose=True,
+                    )
+            live["out", j] = turned
+
+        def take_out_and_store(j, part):
+            tiles = slice(part.start // P, part.stop // P)
             result = work.tile([P, M_TILES, P], F32, name="result")
-            nc.vector.tensor_add(out=result[:], in0=live["diff", j][:], in1=live["rows", CAND, j])
-            nc.sync.dma_start(out=out_tiles[:, :, j * P : (j + 1) * P], in_=result[:])
+            nc.scalar.copy(out=result[:, tiles, :], in_=live["out", j][:, part].rearrange("p (m n) -> p m n", n=P))
+            nc.sync.dma_start(out=out_tiles[:, tiles, j * P : (j + 1) * P], in_=result[:, tiles, :])
 
-        start_sigmoid_gates(0)
-        row_factors(h_side)
-        load_table_of(FUNC.Sigmoid)
-        normalise_h(0, M_TILES)
-        for j in range(1, H_LEAD):
-            normalise_h(j, M_TILES // 2)
-        for j in range(1, X_LEAD):
-            start_sigmoid_gates(j)
-        turn_h(0)
+        H_RESET, H_CAND, H_UPDATE, X_CAND, HX, BACK = 0, 1, 2, 3, 4, 5
 
-        for j in range(J_TILES + 1):
-            gates_now = j < J_TILES
-            blend_now = j >= 1
-            turn_next = j + 1 < J_TILES
-            if gates_now:
-                turn_x_candidate(j)
-            if blend_now:
-                turn_back(j - 1)
-            if gates_now:
-                start_candidate(j)
-                finish_sigmoid_gate(RESET, j)
-                finish_sigmoid_gate(UPDATE, j)
-            if j + H_LEAD < J_TILES:
-                normalise_h(j + H_LEAD, M_TILES // 2)
-            if blend_now:
-                blend_subtract(j - 1)
-            if j + X_LEAD < J_TILES:
-                start_sigmoid_gates(j + X_LEAD)
-            if gates_now:
-                apply_reset(j)
-            if blend_now:
-                blend_scale(j - 1)
-            if gates_now:
-                finish_candidate(j)
-            if blend_now:
-                blend_add_and_store(j - 1)
-            if turn_next:
-                turn_h(j + 1)
+        last = J_TILES - 1
+        turn_h_gate(CAND, 0, bank(H_CAND))
+        turn_h_gate(RESET, 0, bank(H_RESET))
+        turn_h_gate(UPDATE, 0, bank(H_UPDATE))
+        for j in range(last + 1):
+            start_candidate(j)
+            add_h_gate(RESET, j)
+            sigmoid_gate(RESET, j)
+            if j >= 1:
+                turn_hx(j - 1, bank(HX, dtype=BF16))
+            if j >= 1:
+                turn_next_gate()
+            if j < last:
+                turn_h_gate(RESET, j + 1, bank(H_RESET))
+                turn_h_gate(CAND, j + 1, bank(H_CAND))
+                apply_reset(nc.gpsimd, j, ALL)
+            if j >= 1:
+                add_x_candidate(j - 1, ALL)
+                finish_candidate(j - 1, ALL)
+            turn_x_gate(CAND, j, bank(X_CAND))
+            add_h_gate(UPDATE, j)
+            sigmoid_gate(UPDATE, j)
+            for _ in range(3 if j == 0 else 1):
+                start_next_gate(V)
+            if j >= 1:
+                blend_subtract(j - 1, ALL)
+                blend_scale(nc.gpsimd, j - 1, ALL)
+            if j >= 2:
+                turn_back(j - 2, bank(BACK), ALL)
+            if j < last:
+                turn_h_gate(UPDATE, j + 1, bank(H_UPDATE))
+            if j >= 2:
+                take_out_and_store(j - 2, ALL)
+        turn_hx(last, bank(HX, dtype=BF16))
+        back = (bank(H_RESET), bank(H_UPDATE))
+        for part in HALVES:
+            apply_reset(nc.vector, last, part)
+            add_x_candidate(last, part)
+            finish_candidate(last, part)
+        turn_back(last - 1, bank(BACK), ALL)
+        take_out_and_store(last - 1, ALL)
+        for part in HALVES:
+            blend_subtract(last, part)
+            blend_scale(nc.vector, last, part)
+        for part, turned in zip(HALVES, back):
+            turn_back(last, turned, part)
+            take_out_and_store(last, part)

@@ -30,7 +30,6 @@ N_TILES = WIDE // P
 STATS = 6
 BANKS = 8
 W_ARRIVES = 3
-LAST_ON_SCALAR = (0, 2)
 NORM_J = 2
 GATE_TILES = 16
 
@@ -75,7 +74,7 @@ def tile_lngrucell_kernel(
             return {
                 "x_dram": x_dram.rearrange("(m p) k -> m p k", p=P),
                 "words_dram": words_dram.rearrange("g p n t -> p g (n t)").bitcast(I32),
-                "scales_dram": scales_dram.bitcast(I32),
+                "scales_u8": scales_dram,
                 "planes": keep.tile([P, WIDE], U8, name="planes_" + label, align_bytes=64),
                 "x_sb": keep.tile([P, M_TILES, HIDDEN], BF16, name="x_" + label),
                 "w_sb": keep.tile([P, K_PASSES, WIDE], U32, name="w_" + label, align_bytes=64),
@@ -97,12 +96,12 @@ def tile_lngrucell_kernel(
         def load_x(side, m):
             nc.sync.dma_start(out=side["x_sb"][:, m, :], in_=side["x_dram"][m])
 
-        def load_scales(side):
+        def load_scales(side, cols=slice(0, WIDE)):
             for quadrant in range(4):
                 first = 32 * quadrant
                 nc.sync.dma_start(
-                    out=side["planes"][first : first + PACK * K_PASSES, :].bitcast(I32),
-                    in_=side["scales_dram"][:, PACK * quadrant : PACK * (quadrant + 1), :],
+                    out=side["planes"][first : first + PACK * K_PASSES, cols].bitcast(I32),
+                    in_=side["scales_u8"][:, PACK * quadrant : PACK * (quadrant + 1), cols].bitcast(I32),
                 )
 
         def load_words(side, c):
@@ -120,11 +119,16 @@ def tile_lngrucell_kernel(
                     in_=vectors[v].rearrange("(t p) -> t p", p=P),
                 )
 
-        for m in range(M_TILES):
-            load_x(x_side, m)
-        load_scales(x_side)
+        load_x(x_side, 0)
+        load_x(x_side, 1)
+        load_scales(x_side, slice(0, 2 * BANK))
+        load_words(x_side, 0)
+        load_x(x_side, 2)
+        load_x(x_side, 3)
         load_vectors()
-        for c in range(CHUNKS):
+        load_words(x_side, 1)
+        load_scales(x_side, slice(2 * BANK, WIDE))
+        for c in range(2, CHUNKS):
             load_words(x_side, c)
             if c == W_ARRIVES - 1:
                 for m in range(M_TILES):
@@ -261,12 +265,12 @@ def tile_lngrucell_kernel(
             nc.scalar.copy(out=place_of(x_side, m, c), in_=by_tile(acc))
             moments(x_side, m, c, place_of(x_side, m, c))
 
-        def normalise_x(m):
+        def normalise(side, m):
             for j in range(0, J_TILES, NORM_J):
-                run = x_side["rows"][:, m, j : j + NORM_J, :, :].rearrange("p j g n -> p (j g n)")
+                run = side["rows"][:, m, j : j + NORM_J, :, :].rearrange("p j g n -> p (j g n)")
                 nc.gpsimd.tensor_scalar(
                     out=run, in0=run,
-                    scalar1=per_row(x_side, "neg_mean", m), scalar2=per_row(x_side, "rstd", m),
+                    scalar1=per_row(side, "neg_mean", m), scalar2=per_row(side, "rstd", m),
                     op0=ALU.add, op1=ALU.mult,
                 )
 
@@ -274,10 +278,14 @@ def tile_lngrucell_kernel(
             mean_and_var(side, m)
             negate_mean(side, slice(m, m + 1))
 
-        for m in range(M_TILES):
+        turn_k(x_side, 0)
+        quantise(x_side, 0)
+        for m in range(1, M_TILES):
             turn_k(x_side, m)
             quantise(x_side, m)
-        for c in range(W_ARRIVES):
+            product_x(m - 1, 0)
+        product_x(M_TILES - 1, 0)
+        for c in range(1, W_ARRIVES):
             for m in range(M_TILES):
                 product_x(m, c)
         vec_bank = turn_vectors()
@@ -291,7 +299,7 @@ def tile_lngrucell_kernel(
             finish_moments(x_side, m)
             if m >= 1:
                 inverse_std(x_side, slice(m - 1, m))
-                normalise_x(m - 1)
+                normalise(x_side, m - 1)
 
         h_acc = {}
         order = (0, 2, 4, 1, 3, 5)
@@ -326,6 +334,9 @@ def tile_lngrucell_kernel(
         ready_gates = [(gate, j) for j in range(J_TILES) for gate in (RESET, UPDATE)]
         spare = [0]
         V, S = nc.vector, nc.scalar
+        ON_VECTOR = ((), (0, 2, 4), (0, 2), (1, 3, 4, 5))
+        PE_ORDER = ((), range(6), range(6), ())
+        GATES_ON = ((), (S, S, S, V), (S, S, S, V))
 
         turned_gates = []
 
@@ -349,38 +360,33 @@ def tile_lngrucell_kernel(
             moments(h_side, 0, order[k], place_of(h_side, 0, order[k]))
             if k == 2:
                 inverse_std(x_side, slice(M_TILES - 1, M_TILES))
-                normalise_x(M_TILES - 1)
+                normalise(x_side, M_TILES - 1)
         finish_moments(h_side, 0)
         for k in range(CHUNKS):
             product_h(1, k)
         finish_moments(h_side, 1)
-        row_factors_h(0)
-        for j in range(0, J_TILES, NORM_J):
-            run = h_side["rows"][:, 0, j : j + NORM_J, :, :].rearrange("p j g n -> p (j g n)")
-            nc.scalar.activation(
-                out=run, in_=run, func=FUNC.Identity,
-                scale=per_row(h_side, "rstd", 0), bias=per_row(h_side, "neg_mean_rstd", 0),
-            )
+        inverse_std(h_side, slice(0, 1))
+        normalise(h_side, 0)
         turn_next_gate()
         turn_next_gate()
         for m in range(1, M_TILES - 1):
             row_factors_h(m)
             for k in range(CHUNKS):
-                take_out_h(m, k)
-                product_h(m + 1, k)
+                take_out_h(m, k, V if k in ON_VECTOR[m] else S)
+            for k in range(CHUNKS):
+                product_h(m + 1, PE_ORDER[m][k])
             finish_moments(h_side, m + 1)
-            for _ in range(2):
-                start_next_gate(S)
-            for _ in range(2):
-                turn_next_gate()
-            for _ in range(2):
-                start_next_gate(V)
-            for _ in range(2):
+            for engine in GATES_ON[m]:
+                if len(turned_gates) == 0:
+                    turn_next_gate()
+                    turn_next_gate()
+                start_next_gate(engine)
+            while len(turned_gates) < 2:
                 turn_next_gate()
         m = M_TILES - 1
         row_factors_h(m)
         for k in range(CHUNKS):
-            take_out_h(m, k, S if k in LAST_ON_SCALAR else V)
+            take_out_h(m, k, V if k in ON_VECTOR[m] else S)
         load_table_of(FUNC.Sigmoid)
 
         def turn_h_gate(gate, j, turned):
@@ -485,7 +491,7 @@ def tile_lngrucell_kernel(
                 start_next_gate(V)
             if j >= 1:
                 blend_subtract(j - 1, ALL)
-                blend_scale(nc.gpsimd, j - 1, ALL)
+                blend_scale(nc.gpsimd if j < last else nc.vector, j - 1, ALL)
             if j >= 2:
                 turn_back(j - 2, bank(BACK), ALL)
             if j < last:

@@ -104,6 +104,8 @@ def tile_lngrucell_kernel(
                     in_=side["scales_u8"][:, PACK * quadrant : PACK * (quadrant + 1), cols].bitcast(I32),
                 )
 
+        order = (0, 2, 4, 1, 3, 5)
+
         def load_words(side, c):
             cols = slice(c * BANK, (c + 1) * BANK)
             nc.sync.dma_start(out=side["w_sb"][:, :, cols].bitcast(I32), in_=side["words_dram"][:, :, cols])
@@ -134,7 +136,7 @@ def tile_lngrucell_kernel(
                 for m in range(M_TILES):
                     load_x(h_side, m)
         load_scales(h_side)
-        for c in range(CHUNKS):
+        for c in order:
             load_words(h_side, c)
 
         vec_cols = keep.tile([P, P], F32, name="vec_cols")
@@ -265,14 +267,16 @@ def tile_lngrucell_kernel(
             nc.scalar.copy(out=place_of(x_side, m, c), in_=by_tile(acc))
             moments(x_side, m, c, place_of(x_side, m, c))
 
-        def normalise(side, m):
+        def normalise(side, m, neg_mean, rstd):
             for j in range(0, J_TILES, NORM_J):
                 run = side["rows"][:, m, j : j + NORM_J, :, :].rearrange("p j g n -> p (j g n)")
                 nc.gpsimd.tensor_scalar(
                     out=run, in0=run,
-                    scalar1=per_row(side, "neg_mean", m), scalar2=per_row(side, "rstd", m),
-                    op0=ALU.add, op1=ALU.mult,
+                    scalar1=neg_mean, scalar2=rstd, op0=ALU.add, op1=ALU.mult,
                 )
+
+        def normalise_x(m):
+            normalise(x_side, m, per_row(x_side, "neg_mean", m), per_row(x_side, "rstd", m))
 
         def finish_moments(side, m):
             mean_and_var(side, m)
@@ -299,10 +303,9 @@ def tile_lngrucell_kernel(
             finish_moments(x_side, m)
             if m >= 1:
                 inverse_std(x_side, slice(m - 1, m))
-                normalise(x_side, m - 1)
+                normalise_x(m - 1)
 
         h_acc = {}
-        order = (0, 2, 4, 1, 3, 5)
 
         def product_h(m, k):
             if m < M_TILES:
@@ -353,20 +356,65 @@ def tile_lngrucell_kernel(
 
         V, S = nc.vector, nc.scalar
 
+        SUM, SQUARES = 0, 1
+        sums = keep.tile([P, 2, CHUNKS], F32, name="sums")
+        neg_guess = keep.tile([P, 1], F32, name="neg_guess")
+        squares_left = list(range(CHUNKS))
+
+        def square_and_sum(count):
+            for _ in range(count):
+                k = squares_left.pop(0)
+                junk = work.tile([P, J_PER_CHUNK, P], BF16, name="junk", bufs=2)
+                nc.scalar.activation(
+                    out=junk[:], in_=place_of(h_side, 0, order[k]), func=FUNC.Square, bias=neg_guess[:],
+                    accum_out=sums[:, SQUARES, k : k + 1],
+                )
+
+        def normalise_from_sums(side, m):
+            half = CHUNKS // 2
+            tile_of = lambda name, width: keep.tile([P, width], F32, name=name)
+            minus_half = tile_of("minus_half", 1)
+            nc.gpsimd.memset(minus_half[:], -0.5)
+            three = keep.tile([P, 2, half], F32, name="three")
+            total = tile_of("total", 2)
+            scaled = tile_of("scaled", 2)
+            off = tile_of("off", 2)
+            var = tile_of("var", 2)
+            factors = tile_of("factors", 2)
+            add = lambda out, in0, in1, op=ALU.add: nc.gpsimd.tensor_tensor(out=out, in0=in0, in1=in1, op=op)
+            add(three[:], sums[:, :, :half], sums[:, :, half:])
+            add(total[:], three[:, :, 0], three[:, :, 1])
+            add(total[:], total[:], three[:, :, 2])
+            nc.gpsimd.tensor_scalar(
+                out=scaled[:], in0=total[:], scalar1=1.0 / WIDE, scalar2=0.0, op0=ALU.mult, op1=ALU.add
+            )
+            add(off[:, 0:1], scaled[:, 0:1], neg_guess[:])
+            add(off[:, 1:2], off[:, 0:1], off[:, 0:1], ALU.mult)
+            add(var[:, 0:1], scaled[:, 1:2], off[:, 1:2], ALU.subtract)
+            nc.gpsimd.tensor_scalar(
+                out=var[:, 1:2], in0=var[:, 0:1], scalar1=EPS, scalar2=1.0, op0=ALU.add, op1=ALU.mult
+            )
+            add(factors[:, 1:2], var[:, 1:2], minus_half[:], ALU.pow)
+            nc.gpsimd.tensor_scalar(
+                out=factors[:, 0:1], in0=scaled[:, 0:1], scalar1=-1.0, scalar2=0.0, op0=ALU.mult, op1=ALU.add
+            )
+            normalise(side, m, factors[:, 0:1], factors[:, 1:2])
+
         for k in range(CHUNKS):
-            acc = bank(k)
+            acc = bank(CHUNKS + k % 2)
             multiply(h_side, 0, order[k], acc)
-            nc.scalar.copy(out=place_of(h_side, 0, order[k]), in_=by_tile(acc))
-            moments(h_side, 0, order[k], place_of(h_side, 0, order[k]))
-            if k == 2:
+            nc.scalar.activation(
+                out=place_of(h_side, 0, order[k]), in_=by_tile(acc), func=FUNC.Copy,
+                accum_out=sums[:, SUM, k : k + 1],
+            )
+            if k == 0:
+                nc.scalar.activation(out=neg_guess[:], in_=sums[:, SUM, 0:1], func=FUNC.Copy, scale=-1.0 / BANK)
+            if k == 3:
                 inverse_std(x_side, slice(M_TILES - 1, M_TILES))
-                normalise(x_side, M_TILES - 1)
-        finish_moments(h_side, 0)
-        for k in range(CHUNKS):
+                normalise_x(M_TILES - 1)
             product_h(1, k)
+        square_and_sum(2)
         finish_moments(h_side, 1)
-        inverse_std(h_side, slice(0, 1))
-        normalise(h_side, 0)
         turn_next_gate()
         turn_next_gate()
         for m in range(1, M_TILES - 1):
@@ -376,6 +424,9 @@ def tile_lngrucell_kernel(
             for k in range(CHUNKS):
                 product_h(m + 1, PE_ORDER[m][k])
             finish_moments(h_side, m + 1)
+            square_and_sum((0, 4, 0)[m])
+            if m == 1:
+                normalise_from_sums(h_side, 0)
             for engine in GATES_ON[m]:
                 if len(turned_gates) == 0:
                     turn_next_gate()

@@ -104,10 +104,8 @@ def tile_lngrucell_kernel(
                     in_=side["scales_u8"][:, PACK * quadrant : PACK * (quadrant + 1), cols].bitcast(I32),
                 )
 
-        order = (0, 2, 4, 1, 3, 5)
-
-        def load_words(side, c):
-            cols = slice(c * BANK, (c + 1) * BANK)
+        def load_words(side, c, count=1):
+            cols = slice(c * BANK, (c + count) * BANK)
             nc.sync.dma_start(out=side["w_sb"][:, :, cols].bitcast(I32), in_=side["words_dram"][:, :, cols])
 
         vectors = (W_gamma, U_gamma, W_beta, U_beta, b)
@@ -130,14 +128,15 @@ def tile_lngrucell_kernel(
         load_vectors()
         load_words(x_side, 1)
         load_scales(x_side, slice(2 * BANK, WIDE))
-        for c in range(2, CHUNKS):
-            load_words(x_side, c)
-            if c == W_ARRIVES - 1:
-                for m in range(M_TILES):
-                    load_x(h_side, m)
+        load_words(x_side, 2)
+        nc.sync.dma_start(
+            out=h_side["x_sb"][:], in_=hx.rearrange("(m p) k -> p m k", p=P)
+        )
+        load_words(x_side, 3)
+        load_words(x_side, 4, 2)
         load_scales(h_side)
-        for c in order:
-            load_words(h_side, c)
+        for c in range(0, CHUNKS, 2):
+            load_words(h_side, c, 2)
 
         vec_cols = keep.tile([P, P], F32, name="vec_cols")
         gamma_w = vec_cols[:, 0 * N_TILES : 1 * N_TILES]
@@ -154,7 +153,11 @@ def tile_lngrucell_kernel(
 
         def keep_vectors(vec_bank):
             nc.vector.tensor_copy(out=vec_cols[:], in_=vec_bank[:])
-            nc.vector.tensor_add(out=shift[:], in0=beta_w, in1=bias_b)
+
+        def add_shifts(first):
+            if first:
+                nc.vector.tensor_add(out=shift[:], in0=beta_w, in1=bias_b)
+                return
             sigmoid_tiles = 2 * J_TILES
             nc.vector.tensor_add(
                 out=shift[:, :sigmoid_tiles], in0=shift[:, :sigmoid_tiles], in1=beta_u[:, :sigmoid_tiles]
@@ -165,7 +168,7 @@ def tile_lngrucell_kernel(
 
         grouped = {}
 
-        def turn_k(side, m):
+        def turn_k(side, m, copy=nc.scalar.copy):
             words = side["x_sb"][:, m, :].bitcast(F32)
             turned = next_bank()
             for g in range(K_PASSES):
@@ -177,7 +180,7 @@ def tile_lngrucell_kernel(
                         identity=identity[:],
                     )
             copied = stage.tile([P, K_PASSES * P * PACK], BF16, name="copied", align_bytes=64)
-            nc.scalar.copy(
+            copy(
                 out=copied[:].bitcast(F32).rearrange("p (g r u) -> p g r u", g=K_PASSES, u=2),
                 in_=turned[:].rearrange("p (g u r) -> p g r u", g=K_PASSES, u=2),
             )
@@ -221,10 +224,8 @@ def tile_lngrucell_kernel(
                 out=side["mean_var"][:, m, :], in_=side["stats"][:, m, :, :].rearrange("p c s -> p (c s)")
             )
 
-        def negate_mean(side, tiles):
-            nc.vector.tensor_scalar_mul(
-                out=side["neg_mean"][:, tiles], in0=side["mean_var"][:, tiles, 0], scalar1=-1.0
-            )
+        def mean_of(side, m):
+            return side["mean_var"][:, m, 0:1]
 
         def inverse_std(side, tiles):
             nc.scalar.activation(
@@ -267,29 +268,29 @@ def tile_lngrucell_kernel(
             nc.scalar.copy(out=place_of(x_side, m, c), in_=by_tile(acc))
             moments(x_side, m, c, place_of(x_side, m, c))
 
-        def normalise(side, m, neg_mean, rstd):
+        def normalise(side, m, mean, rstd):
             for j in range(0, J_TILES, NORM_J):
                 run = side["rows"][:, m, j : j + NORM_J, :, :].rearrange("p j g n -> p (j g n)")
                 nc.gpsimd.tensor_scalar(
                     out=run, in0=run,
-                    scalar1=neg_mean, scalar2=rstd, op0=ALU.add, op1=ALU.mult,
+                    scalar1=mean, scalar2=rstd, op0=ALU.subtract, op1=ALU.mult,
                 )
 
         def normalise_x(m):
-            normalise(x_side, m, per_row(x_side, "neg_mean", m), per_row(x_side, "rstd", m))
+            normalise(x_side, m, mean_of(x_side, m), per_row(x_side, "rstd", m))
 
-        def finish_moments(side, m):
-            mean_and_var(side, m)
-            negate_mean(side, slice(m, m + 1))
-
-        turn_k(x_side, 0)
-        quantise(x_side, 0)
-        for m in range(1, M_TILES):
-            turn_k(x_side, m)
-            quantise(x_side, m)
-            product_x(m - 1, 0)
-        product_x(M_TILES - 1, 0)
-        for c in range(1, W_ARRIVES):
+        pairs = ((0, 1), (2, 3))
+        for pair in pairs:
+            for m in pair:
+                turn_k(x_side, m)
+            for m in pair:
+                quantise(x_side, m)
+            if pair == pairs[0]:
+                for m in pair:
+                    product_x(m, 0)
+        for m, c in ((0, 1), (1, 1), (2, 0), (3, 0), (2, 1), (3, 1)):
+            product_x(m, c)
+        for c in range(2, W_ARRIVES):
             for m in range(M_TILES):
                 product_x(m, c)
         vec_bank = turn_vectors()
@@ -300,35 +301,46 @@ def tile_lngrucell_kernel(
         for m in range(M_TILES):
             for c in range(W_ARRIVES, CHUNKS):
                 product_x(m, c)
-            finish_moments(x_side, m)
+                if m == 0 and c < W_ARRIVES + 2:
+                    add_shifts(first=c == W_ARRIVES)
+                if m >= 1 and c == W_ARRIVES:
+                    mean_and_var(x_side, m - 1)
             if m >= 1:
                 inverse_std(x_side, slice(m - 1, m))
                 normalise_x(m - 1)
 
         h_acc = {}
+        natural = range(CHUNKS)
+        by_halves = (0, 2, 4, 1, 3, 5)
+
+        def chunk(m, k):
+            return (by_halves if m == M_TILES - 1 else natural)[k]
+
 
         def product_h(m, k):
             if m < M_TILES:
                 h_acc[m, k] = bank(k)
-                multiply(h_side, m, order[k], h_acc[m, k])
-                moments(h_side, m, order[k], h_acc[m, k][:])
+                multiply(h_side, m, chunk(m, k), h_acc[m, k])
+                moments(h_side, m, chunk(m, k), h_acc[m, k][:])
 
         def take_out_h(m, k, engine=None):
             if engine is nc.vector:
                 nc.vector.tensor_scalar(
-                    out=place_of(h_side, m, order[k]), in0=by_tile(h_acc[m, k]),
-                    scalar1=per_row(h_side, "neg_mean", m), scalar2=per_row(h_side, "rstd", m),
-                    op0=ALU.add, op1=ALU.mult,
+                    out=place_of(h_side, m, chunk(m, k)), in0=by_tile(h_acc[m, k]),
+                    scalar1=mean_of(h_side, m), scalar2=per_row(h_side, "rstd", m),
+                    op0=ALU.subtract, op1=ALU.mult,
                 )
                 return
             nc.scalar.activation(
-                out=place_of(h_side, m, order[k]), in_=by_tile(h_acc[m, k]), func=FUNC.Identity,
+                out=place_of(h_side, m, chunk(m, k)), in_=by_tile(h_acc[m, k]), func=FUNC.Identity,
                 scale=per_row(h_side, "rstd", m), bias=per_row(h_side, "neg_mean_rstd", m),
             )
 
         def row_factors_h(m):
-            tile = slice(m, m + 1)
-            inverse_std(h_side, tile)
+            inverse_std(h_side, slice(m, m + 1))
+            nc.scalar.activation(
+                out=per_row(h_side, "neg_mean", m), in_=mean_of(h_side, m), func=FUNC.Copy, scale=-1.0
+            )
             nc.scalar.activation(
                 out=per_row(h_side, "neg_mean_rstd", m), in_=per_row(h_side, "neg_mean", m), func=FUNC.Copy,
                 scale=per_row(h_side, "rstd", m),
@@ -337,8 +349,7 @@ def tile_lngrucell_kernel(
         ready_gates = [(gate, j) for j in range(J_TILES) for gate in (RESET, UPDATE)]
         spare = [0]
         V, S = nc.vector, nc.scalar
-        ON_VECTOR = ((), (0, 2, 4), (0, 2), (1, 3, 4, 5))
-        PE_ORDER = ((), range(6), range(6), ())
+        ON_VECTOR = ((), (0, 2, 4), (1, 3), (1, 3, 4, 5))
         GATES_ON = ((), (S, S, S, V), (S, S, S, V))
 
         turned_gates = []
@@ -366,7 +377,7 @@ def tile_lngrucell_kernel(
                 k = squares_left.pop(0)
                 junk = work.tile([P, J_PER_CHUNK, P], BF16, name="junk", bufs=2)
                 nc.scalar.activation(
-                    out=junk[:], in_=place_of(h_side, 0, order[k]), func=FUNC.Square, bias=neg_guess[:],
+                    out=junk[:], in_=place_of(h_side, 0, k), func=FUNC.Square, bias=neg_guess[:],
                     accum_out=sums[:, SQUARES, k : k + 1],
                 )
 
@@ -380,7 +391,7 @@ def tile_lngrucell_kernel(
             scaled = tile_of("scaled", 2)
             off = tile_of("off", 2)
             var = tile_of("var", 2)
-            factors = tile_of("factors", 2)
+            rstd = tile_of("rstd_from_sums", 1)
             add = lambda out, in0, in1, op=ALU.add: nc.gpsimd.tensor_tensor(out=out, in0=in0, in1=in1, op=op)
             add(three[:], sums[:, :, :half], sums[:, :, half:])
             add(total[:], three[:, :, 0], three[:, :, 1])
@@ -394,17 +405,14 @@ def tile_lngrucell_kernel(
             nc.gpsimd.tensor_scalar(
                 out=var[:, 1:2], in0=var[:, 0:1], scalar1=EPS, scalar2=1.0, op0=ALU.add, op1=ALU.mult
             )
-            add(factors[:, 1:2], var[:, 1:2], minus_half[:], ALU.pow)
-            nc.gpsimd.tensor_scalar(
-                out=factors[:, 0:1], in0=scaled[:, 0:1], scalar1=-1.0, scalar2=0.0, op0=ALU.mult, op1=ALU.add
-            )
-            normalise(side, m, factors[:, 0:1], factors[:, 1:2])
+            add(rstd[:], var[:, 1:2], minus_half[:], ALU.pow)
+            normalise(side, m, scaled[:, 0:1], rstd[:])
 
         for k in range(CHUNKS):
             acc = bank(CHUNKS + k % 2)
-            multiply(h_side, 0, order[k], acc)
+            multiply(h_side, 0, k, acc)
             nc.scalar.activation(
-                out=place_of(h_side, 0, order[k]), in_=by_tile(acc), func=FUNC.Copy,
+                out=place_of(h_side, 0, k), in_=by_tile(acc), func=FUNC.Copy,
                 accum_out=sums[:, SUM, k : k + 1],
             )
             if k == 0:
@@ -413,18 +421,18 @@ def tile_lngrucell_kernel(
                 inverse_std(x_side, slice(M_TILES - 1, M_TILES))
                 normalise_x(M_TILES - 1)
             product_h(1, k)
-        square_and_sum(2)
-        finish_moments(h_side, 1)
-        turn_next_gate()
-        turn_next_gate()
+            if k == 0:
+                mean_and_var(x_side, M_TILES - 1)
+        square_and_sum(1)
+        mean_and_var(h_side, 1)
         for m in range(1, M_TILES - 1):
             row_factors_h(m)
             for k in range(CHUNKS):
                 take_out_h(m, k, V if k in ON_VECTOR[m] else S)
             for k in range(CHUNKS):
-                product_h(m + 1, PE_ORDER[m][k])
-            finish_moments(h_side, m + 1)
-            square_and_sum((0, 4, 0)[m])
+                product_h(m + 1, k)
+            mean_and_var(h_side, m + 1)
+            square_and_sum((0, 5, 0)[m])
             if m == 1:
                 normalise_from_sums(h_side, 0)
             for engine in GATES_ON[m]:
@@ -540,21 +548,23 @@ def tile_lngrucell_kernel(
             sigmoid_gate(UPDATE, j)
             for _ in range(3 if j == 0 else 1):
                 start_next_gate(V)
-            if j >= 1:
+            if 1 <= j < last:
                 blend_subtract(j - 1, ALL)
-                blend_scale(nc.gpsimd if j < last else nc.vector, j - 1, ALL)
+                blend_scale(nc.gpsimd, j - 1, ALL)
             if j >= 2:
                 turn_back(j - 2, bank(BACK), ALL)
             if j < last:
                 turn_h_gate(UPDATE, j + 1, bank(H_UPDATE))
             if j >= 2:
                 take_out_and_store(j - 2, ALL)
-        turn_hx(last, bank(HX, dtype=BF16))
         back = (bank(H_RESET), bank(H_UPDATE))
         for part in HALVES:
             apply_reset(nc.vector, last, part)
             add_x_candidate(last, part)
             finish_candidate(last, part)
+        blend_subtract(last - 1, ALL)
+        blend_scale(nc.vector, last - 1, ALL)
+        turn_hx(last, bank(HX, dtype=BF16))
         turn_back(last - 1, bank(BACK), ALL)
         take_out_and_store(last - 1, ALL)
         for part in HALVES:

@@ -129,11 +129,9 @@ def tile_lngrucell_kernel(
         load_words(x_side, 1)
         load_scales(x_side, slice(2 * BANK, WIDE))
         load_words(x_side, 2)
-        nc.sync.dma_start(
-            out=h_side["x_sb"][:], in_=hx.rearrange("(m p) k -> p m k", p=P)
-        )
         load_words(x_side, 3)
         load_words(x_side, 4, 2)
+        nc.sync.dma_start(out=h_side["x_sb"][:], in_=hx.rearrange("(m p) k -> p m k", p=P))
         load_scales(h_side)
         for c in range(0, CHUNKS, 2):
             load_words(h_side, c, 2)
@@ -227,10 +225,13 @@ def tile_lngrucell_kernel(
         def mean_of(side, m):
             return side["mean_var"][:, m, 0:1]
 
-        def inverse_std(side, tiles):
+        def row_factors(side, m):
             nc.scalar.activation(
-                out=side["rstd"][:, tiles], in_=side["mean_var"][:, tiles, 1],
+                out=per_row(side, "rstd", m), in_=side["mean_var"][:, m, 1:2],
                 func=FUNC.Abs_reciprocal_sqrt, bias=EPS,
+            )
+            nc.scalar.activation(
+                out=per_row(side, "neg_mean", m), in_=mean_of(side, m), func=FUNC.Copy, scale=-1.0
             )
 
         RESET, UPDATE, CAND = 1, 0, 2
@@ -268,16 +269,16 @@ def tile_lngrucell_kernel(
             nc.scalar.copy(out=place_of(x_side, m, c), in_=by_tile(acc))
             moments(x_side, m, c, place_of(x_side, m, c))
 
-        def normalise(side, m, mean, rstd):
+        def normalise(side, m, neg_mean, rstd):
             for j in range(0, J_TILES, NORM_J):
                 run = side["rows"][:, m, j : j + NORM_J, :, :].rearrange("p j g n -> p (j g n)")
                 nc.gpsimd.tensor_scalar(
                     out=run, in0=run,
-                    scalar1=mean, scalar2=rstd, op0=ALU.subtract, op1=ALU.mult,
+                    scalar1=neg_mean, scalar2=rstd, op0=ALU.add, op1=ALU.mult,
                 )
 
         def normalise_x(m):
-            normalise(x_side, m, mean_of(x_side, m), per_row(x_side, "rstd", m))
+            normalise(x_side, m, per_row(x_side, "neg_mean", m), per_row(x_side, "rstd", m))
 
         pairs = ((0, 1), (2, 3))
         for pair in pairs:
@@ -293,21 +294,22 @@ def tile_lngrucell_kernel(
         for c in range(2, W_ARRIVES):
             for m in range(M_TILES):
                 product_x(m, c)
-        vec_bank = turn_vectors()
-        for m in range(M_TILES):
-            turn_k(h_side, m)
-            quantise(h_side, m)
-        keep_vectors(vec_bank)
         for m in range(M_TILES):
             for c in range(W_ARRIVES, CHUNKS):
                 product_x(m, c)
-                if m == 0 and c < W_ARRIVES + 2:
-                    add_shifts(first=c == W_ARRIVES)
+                if m == 1 + 1 and c > W_ARRIVES:
+                    add_shifts(first=c == W_ARRIVES + 1)
                 if m >= 1 and c == W_ARRIVES:
                     mean_and_var(x_side, m - 1)
             if m >= 1:
-                inverse_std(x_side, slice(m - 1, m))
+                row_factors(x_side, m - 1)
                 normalise_x(m - 1)
+            if m == 1:
+                vec_bank = turn_vectors()
+                for m_h in range(M_TILES):
+                    turn_k(h_side, m_h)
+                    quantise(h_side, m_h)
+                keep_vectors(vec_bank)
 
         h_acc = {}
         natural = range(CHUNKS)
@@ -337,10 +339,7 @@ def tile_lngrucell_kernel(
             )
 
         def row_factors_h(m):
-            inverse_std(h_side, slice(m, m + 1))
-            nc.scalar.activation(
-                out=per_row(h_side, "neg_mean", m), in_=mean_of(h_side, m), func=FUNC.Copy, scale=-1.0
-            )
+            row_factors(h_side, m)
             nc.scalar.activation(
                 out=per_row(h_side, "neg_mean_rstd", m), in_=per_row(h_side, "neg_mean", m), func=FUNC.Copy,
                 scale=per_row(h_side, "rstd", m),
@@ -392,6 +391,7 @@ def tile_lngrucell_kernel(
             off = tile_of("off", 2)
             var = tile_of("var", 2)
             rstd = tile_of("rstd_from_sums", 1)
+            neg_mean = tile_of("neg_mean_from_sums", 1)
             add = lambda out, in0, in1, op=ALU.add: nc.gpsimd.tensor_tensor(out=out, in0=in0, in1=in1, op=op)
             add(three[:], sums[:, :, :half], sums[:, :, half:])
             add(total[:], three[:, :, 0], three[:, :, 1])
@@ -406,7 +406,10 @@ def tile_lngrucell_kernel(
                 out=var[:, 1:2], in0=var[:, 0:1], scalar1=EPS, scalar2=1.0, op0=ALU.add, op1=ALU.mult
             )
             add(rstd[:], var[:, 1:2], minus_half[:], ALU.pow)
-            normalise(side, m, scaled[:, 0:1], rstd[:])
+            nc.gpsimd.tensor_scalar(
+                out=neg_mean[:], in0=scaled[:, 0:1], scalar1=-1.0, scalar2=0.0, op0=ALU.mult, op1=ALU.add
+            )
+            normalise(side, m, neg_mean[:], rstd[:])
 
         for k in range(CHUNKS):
             acc = bank(CHUNKS + k % 2)
@@ -418,7 +421,7 @@ def tile_lngrucell_kernel(
             if k == 0:
                 nc.scalar.activation(out=neg_guess[:], in_=sums[:, SUM, 0:1], func=FUNC.Copy, scale=-1.0 / BANK)
             if k == 3:
-                inverse_std(x_side, slice(M_TILES - 1, M_TILES))
+                row_factors(x_side, M_TILES - 1)
                 normalise_x(M_TILES - 1)
             product_h(1, k)
             if k == 0:

from contextlib import ExitStack

import concourse.mybir as mybir
from concourse.masks import make_identity

F32 = mybir.dt.float32
BF16 = mybir.dt.bfloat16
I32 = mybir.dt.int32
U32 = mybir.dt.uint32
U8 = mybir.dt.uint8
FP8X4 = mybir.dt.float8_e4m3fn_x4
ALU = mybir.AluOpType
FUNC = mybir.ActivationFunctionType

P = 128
PACK = 4
BATCH = 512
HIDDEN = 1024
GATES = 3
WIDE = GATES * HIDDEN
EPS = 1e-5

M_TILES = BATCH // P
K_PASSES = HIDDEN // (P * PACK)
BANK = 512
CHUNKS = WIDE // BANK
J_TILES = HIDDEN // P
J_PER_CHUNK = BANK // P
N_TILES = WIDE // P
STATS = 6
BANKS = 8
W_ARRIVES = 3
NORM_J = 2
GATE_TILES = 16

FLOPS = 2 * 2 * BATCH * HIDDEN * WIDE


def tile_lngrucell_kernel(
    tc, x_in, hx, W_words, W_scales, U_words, U_scales, b, W_gamma, W_beta, U_gamma, U_beta, out
):
    nc = tc.nc
    with ExitStack() as ctx:
        keep = ctx.enter_context(tc.tile_pool(name="keep", bufs=1))
        stage = ctx.enter_context(tc.tile_pool(name="stage", bufs=2))
        work = ctx.enter_context(tc.tile_pool(name="work", bufs=3))
        psum = ctx.enter_context(tc.psum_pool(name="psum", bufs=1))
        ctx.enter_context(tc.manual_schedule())

        def bank(k, width=BANK, dtype=F32):
            return psum.tile([P, width], dtype, name="bank", tag="bank%d" % k)

        turns = [0]

        def next_bank(width=BANK, dtype=F32):
            turns[0] += 1
            return bank((turns[0] - 1) % BANKS, width, dtype)

        identity = keep.tile([P, P], F32, name="identity")
        make_identity(nc, identity[:])
        identity_bf16 = keep.tile([P, P], BF16, name="identity_bf16")
        make_identity(nc, identity_bf16[:])

        one = keep.tile([P, 1], F32, name="one")
        nc.vector.memset(one[:], 1.0)
        warmed = keep.tile([P, 1], F32, name="warmed")

        def load_table_of(func):
            nc.scalar.activation(out=warmed[:], in_=one[:], func=func)

        load_table_of(FUNC.Abs_reciprocal_sqrt)

        def make_side(label, x_dram, words_dram, scales_dram):
            return {
                "x_dram": x_dram.rearrange("(m p) k -> m p k", p=P),
                "words_dram": words_dram.rearrange("g p n t -> p g (n t)").bitcast(I32),
                "scales_u8": scales_dram,
                "planes": keep.tile([P, WIDE], U8, name="planes_" + label, align_bytes=64),
                "x_sb": keep.tile([P, M_TILES, HIDDEN], BF16, name="x_" + label),
                "w_sb": keep.tile([P, K_PASSES, WIDE], U32, name="w_" + label, align_bytes=64),
                "codes": keep.tile([P, M_TILES, K_PASSES * P], U32, name="codes_" + label, align_bytes=64),
                "x_scales": keep.tile([P, M_TILES, K_PASSES * P], U8, name="xs_" + label, align_bytes=64),
                "rows": keep.tile([P, M_TILES, J_TILES, GATES, P], F32, name="rows_" + label),
                "stats": keep.tile([P, M_TILES, CHUNKS, STATS], F32, name="stats_" + label),
                "mean_var": keep.tile([P, M_TILES, 2], F32, name="mv_" + label),
                "neg_mean": keep.tile([P, M_TILES], F32, name="nm_" + label),
                "rstd": keep.tile([P, M_TILES], F32, name="rstd_" + label),
                "neg_mean_rstd": keep.tile([P, M_TILES], F32, name="nmr_" + label),
            }

        x_side = make_side("x", x_in, W_words, W_scales)
        h_side = make_side("h", hx, U_words, U_scales)
        for side in (x_side, h_side):
            nc.vector.memset(side["planes"][:].bitcast(I32), 0)

        def load_x(side, m):
            nc.sync.dma_start(out=side["x_sb"][:, m, :], in_=side["x_dram"][m])

        def load_scales(side, cols=slice(0, WIDE)):
            for quadrant in range(4):
                first = 32 * quadrant
                nc.sync.dma_start(
                    out=side["planes"][first : first + PACK * K_PASSES, cols].bitcast(I32),
                    in_=side["scales_u8"][:, PACK * quadrant : PACK * (quadrant + 1), cols].bitcast(I32),
                )

        def load_words(side, c, count=1):
            cols = slice(c * BANK, (c + count) * BANK)
            nc.sync.dma_start(out=side["w_sb"][:, :, cols].bitcast(I32), in_=side["words_dram"][:, :, cols])

        vectors = (W_gamma, U_gamma, W_beta, U_beta, b)
        vec_rows = keep.tile([P, P], BF16, name="vec_rows")
        nc.vector.memset(vec_rows[:].bitcast(I32), 0)

        def load_vectors():
            for v in range(len(vectors)):
                nc.gpsimd.dma_start(
                    out=vec_rows[v * N_TILES : (v + 1) * N_TILES, :],
                    in_=vectors[v].rearrange("(t p) -> t p", p=P),
                )

        load_x(x_side, 0)
        load_x(x_side, 1)
        load_scales(x_side, slice(0, 2 * BANK))
        load_words(x_side, 0)
        load_x(x_side, 2)
        load_x(x_side, 3)
        load_vectors()
        load_words(x_side, 1)
        load_scales(x_side, slice(2 * BANK, WIDE))
        load_words(x_side, 2)
        load_words(x_side, 3)
        load_words(x_side, 4, 2)
        nc.sync.dma_start(out=h_side["x_sb"][:], in_=hx.rearrange("(m p) k -> p m k", p=P))
        load_scales(h_side)
        for c in range(0, CHUNKS, 2):
            load_words(h_side, c, 2)

        vec_cols = keep.tile([P, P], F32, name="vec_cols")
        gamma_w = vec_cols[:, 0 * N_TILES : 1 * N_TILES]
        gamma_u = vec_cols[:, 1 * N_TILES : 2 * N_TILES]
        beta_w = vec_cols[:, 2 * N_TILES : 3 * N_TILES]
        beta_u = vec_cols[:, 3 * N_TILES : 4 * N_TILES]
        bias_b = vec_cols[:, 4 * N_TILES : 5 * N_TILES]
        shift = keep.tile([P, N_TILES], F32, name="shift")

        def turn_vectors():
            vec_bank = next_bank(P, BF16)
            nc.tensor.transpose(out=vec_bank[:], in_=vec_rows[:], identity=identity_bf16[:])
            return vec_bank

        def keep_vectors(vec_bank):
            nc.vector.tensor_copy(out=vec_cols[:], in_=vec_bank[:])

        def add_shifts(first):
            if first:
                nc.vector.tensor_add(out=shift[:], in0=beta_w, in1=bias_b)
                return
            sigmoid_tiles = 2 * J_TILES
            nc.vector.tensor_add(
                out=shift[:, :sigmoid_tiles], in0=shift[:, :sigmoid_tiles], in1=beta_u[:, :sigmoid_tiles]
            )

        def column(table, t):
            return table[:, t : t + 1]

        grouped = {}

        def turn_k(side, m, copy=nc.scalar.copy):
            words = side["x_sb"][:, m, :].bitcast(F32)
            turned = next_bank()
            for g in range(K_PASSES):
                for u in range(2):
                    piece = 2 * g + u
                    nc.tensor.transpose(
                        out=turned[:, piece * P : (piece + 1) * P],
                        in_=words[:, 2 * P * g + u : 2 * P * (g + 1) : 2],
                        identity=identity[:],
                    )
            copied = stage.tile([P, K_PASSES * P * PACK], BF16, name="copied", align_bytes=64)
            copy(
                out=copied[:].bitcast(F32).rearrange("p (g r u) -> p g r u", g=K_PASSES, u=2),
                in_=turned[:].rearrange("p (g u r) -> p g r u", g=K_PASSES, u=2),
            )
            grouped[m] = copied

        def quantise(side, m):
            nc.vector.quantize_mx(
                out=side["codes"][:, m, :].bitcast(FP8X4), scales=side["x_scales"][:, m, :], in_=grouped[m][:]
            )

        def multiply(side, m, c, acc):
            cols = slice(c * BANK, (c + 1) * BANK)
            for g in range(K_PASSES):
                batch_rows = slice(g * P, (g + 1) * P)
                nc.tensor.matmul_mx(
                    out=acc[:],
                    lhsT=side["codes"][:, m, batch_rows].bitcast(FP8X4),
                    lhsT_scale=side["x_scales"][:, m, batch_rows],
                    rhs=side["w_sb"][:, g, cols].bitcast(FP8X4),
                    rhs_scale=side["planes"][PACK * g : P, cols],
                    start=(g == 0),
                    stop=(g == K_PASSES - 1),
                )

        def place_of(side, m, c):
            gate = c // (CHUNKS // GATES)
            j_first = J_PER_CHUNK * (c % (CHUNKS // GATES))
            return side["rows"][:, m, j_first : j_first + J_PER_CHUNK, gate, :]

        def by_tile(acc):
            return acc[:].rearrange("p (j n) -> p j n", n=P)

        def per_row(side, what, m):
            return side[what][:, m : m + 1]

        def moments(side, m, c, source):
            nc.vector.bn_stats(out=side["stats"][:, m, c, :], in_=source)

        def mean_and_var(side, m):
            nc.vector.bn_aggr(
                out=side["mean_var"][:, m, :], in_=side["stats"][:, m, :, :].rearrange("p c s -> p (c s)")
            )

        def mean_of(side, m):
            return side["mean_var"][:, m, 0:1]

        def row_factors(side, m):
            nc.scalar.activation(
                out=per_row(side, "rstd", m), in_=side["mean_var"][:, m, 1:2],
                func=FUNC.Abs_reciprocal_sqrt, bias=EPS,
            )
            nc.scalar.activation(
                out=per_row(side, "neg_mean", m), in_=mean_of(side, m), func=FUNC.Copy, scale=-1.0
            )

        RESET, UPDATE, CAND = 1, 0, 2
        live = {}

        def turn(side, gate, j, turned):
            for m in range(M_TILES):
                nc.tensor.transpose(
                    out=turned[:, m * P : (m + 1) * P],
                    in_=side["rows"][:, m, j, gate, :],
                    identity=identity[:],
                )
            return turned

        def scale_and_shift(engine, out, in_, scale, bias):
            if engine is nc.scalar:
                nc.scalar.activation(out=out, in_=in_, func=FUNC.Identity, scale=scale, bias=bias)
            else:
                nc.vector.tensor_scalar(
                    out=out, in0=in_, scalar1=scale, scalar2=bias, op0=ALU.mult, op1=ALU.add
                )

        def turn_x_gate(gate, j, turned):
            live["x", gate, j] = turn(x_side, gate, j, turned)

        def start_gate(engine, gate, j):
            t = gate * J_TILES + j
            value = work.tile([P, BATCH], F32, name="gate", bufs=GATE_TILES)
            scale_and_shift(engine, value[:], live["x", gate, j][:], column(gamma_w, t), column(shift, t))
            live[gate, j] = value

        def product_x(m, c):
            acc = next_bank()
            multiply(x_side, m, c, acc)
            nc.scalar.copy(out=place_of(x_side, m, c), in_=by_tile(acc))
            moments(x_side, m, c, place_of(x_side, m, c))

        def normalise(side, m, neg_mean, rstd):
            for j in range(0, J_TILES, NORM_J):
                run = side["rows"][:, m, j : j + NORM_J, :, :].rearrange("p j g n -> p (j g n)")
                nc.gpsimd.tensor_scalar(
                    out=run, in0=run,
                    scalar1=neg_mean, scalar2=rstd, op0=ALU.add, op1=ALU.mult,
                )

        def normalise_x(m):
            normalise(x_side, m, per_row(x_side, "neg_mean", m), per_row(x_side, "rstd", m))

        pairs = ((0, 1), (2, 3))
        for pair in pairs:
            for m in pair:
                turn_k(x_side, m)
            for m in pair:
                quantise(x_side, m)
            if pair == pairs[0]:
                for m in pair:
                    product_x(m, 0)
        for m, c in ((0, 1), (1, 1), (2, 0), (3, 0), (2, 1), (3, 1)):
            product_x(m, c)
        for c in range(2, W_ARRIVES):
            for m in range(M_TILES):
                product_x(m, c)
        for m in range(M_TILES):
            for c in range(W_ARRIVES, CHUNKS):
                product_x(m, c)
                if m == 1 + 1 and c > W_ARRIVES:
                    add_shifts(first=c == W_ARRIVES + 1)
                if m >= 1 and c == W_ARRIVES:
                    mean_and_var(x_side, m - 1)
            if m >= 1:
                row_factors(x_side, m - 1)
                normalise_x(m - 1)
            if m == 1:
                vec_bank = turn_vectors()
                for m_h in range(M_TILES):
                    turn_k(h_side, m_h)
                    quantise(h_side, m_h)
                keep_vectors(vec_bank)

        h_acc = {}
        natural = range(CHUNKS)
        by_halves = (0, 2, 4, 1, 3, 5)

        def chunk(m, k):
            return (by_halves if m == M_TILES - 1 else natural)[k]


        def product_h(m, k):
            if m < M_TILES:
                h_acc[m, k] = bank(k)
                multiply(h_side, m, chunk(m, k), h_acc[m, k])
                moments(h_side, m, chunk(m, k), h_acc[m, k][:])

        def take_out_h(m, k, engine=None):
            if engine is nc.vector:
                nc.vector.tensor_scalar(
                    out=place_of(h_side, m, chunk(m, k)), in0=by_tile(h_acc[m, k]),
                    scalar1=mean_of(h_side, m), scalar2=per_row(h_side, "rstd", m),
                    op0=ALU.subtract, op1=ALU.mult,
                )
                return
            nc.scalar.activation(
                out=place_of(h_side, m, chunk(m, k)), in_=by_tile(h_acc[m, k]), func=FUNC.Identity,
                scale=per_row(h_side, "rstd", m), bias=per_row(h_side, "neg_mean_rstd", m),
            )

        def row_factors_h(m):
            row_factors(h_side, m)
            nc.scalar.activation(
                out=per_row(h_side, "neg_mean_rstd", m), in_=per_row(h_side, "neg_mean", m), func=FUNC.Copy,
                scale=per_row(h_side, "rstd", m),
            )

        ready_gates = [(gate, j) for j in range(J_TILES) for gate in (RESET, UPDATE)]
        spare = [0]
        V, S = nc.vector, nc.scalar
        ON_VECTOR = ((), (0, 2, 4), (1, 3), (1, 3, 4, 5))
        GATES_ON = ((), (S, S, S, V), (S, S, S, V))

        turned_gates = []

        def turn_next_gate(k=None):
            if ready_gates:
                gate, j = ready_gates.pop(0)
                spare[0] += 1
                turn_x_gate(gate, j, bank(CHUNKS + spare[0] % 2 if k is None else k))
                turned_gates.append((gate, j))

        def start_next_gate(engine):
            if turned_gates:
                start_gate(engine, *turned_gates.pop(0))

        V, S = nc.vector, nc.scalar

        SUM, SQUARES = 0, 1
        sums = keep.tile([P, 2, CHUNKS], F32, name="sums")
        neg_guess = keep.tile([P, 1], F32, name="neg_guess")
        squares_left = list(range(CHUNKS))

        def square_and_sum(count):
            for _ in range(count):
                k = squares_left.pop(0)
                junk = work.tile([P, J_PER_CHUNK, P], BF16, name="junk", bufs=2)
                nc.scalar.activation(
                    out=junk[:], in_=place_of(h_side, 0, k), func=FUNC.Square, bias=neg_guess[:],
                    accum_out=sums[:, SQUARES, k : k + 1],
                )

        def normalise_from_sums(side, m):
            half = CHUNKS // 2
            tile_of = lambda name, width: keep.tile([P, width], F32, name=name)
            minus_half = tile_of("minus_half", 1)
            nc.gpsimd.memset(minus_half[:], -0.5)
            three = keep.tile([P, 2, half], F32, name="three")
            total = tile_of("total", 2)
            scaled = tile_of("scaled", 2)
            off = tile_of("off", 2)
            var = tile_of("var", 2)
            rstd = tile_of("rstd_from_sums", 1)
            neg_mean = tile_of("neg_mean_from_sums", 1)
            add = lambda out, in0, in1, op=ALU.add: nc.gpsimd.tensor_tensor(out=out, in0=in0, in1=in1, op=op)
            add(three[:], sums[:, :, :half], sums[:, :, half:])
            add(total[:], three[:, :, 0], three[:, :, 1])
            add(total[:], total[:], three[:, :, 2])
            nc.gpsimd.tensor_scalar(
                out=scaled[:], in0=total[:], scalar1=1.0 / WIDE, scalar2=0.0, op0=ALU.mult, op1=ALU.add
            )
            add(off[:, 0:1], scaled[:, 0:1], neg_guess[:])
            add(off[:, 1:2], off[:, 0:1], off[:, 0:1], ALU.mult)
            add(var[:, 0:1], scaled[:, 1:2], off[:, 1:2], ALU.subtract)
            nc.gpsimd.tensor_scalar(
                out=var[:, 1:2], in0=var[:, 0:1], scalar1=EPS, scalar2=1.0, op0=ALU.add, op1=ALU.mult
            )
            add(rstd[:], var[:, 1:2], minus_half[:], ALU.pow)
            nc.gpsimd.tensor_scalar(
                out=neg_mean[:], in0=scaled[:, 0:1], scalar1=-1.0, scalar2=0.0, op0=ALU.mult, op1=ALU.add
            )
            normalise(side, m, neg_mean[:], rstd[:])

        for k in range(CHUNKS):
            acc = bank(CHUNKS + k % 2)
            multiply(h_side, 0, k, acc)
            nc.scalar.activation(
                out=place_of(h_side, 0, k), in_=by_tile(acc), func=FUNC.Copy,
                accum_out=sums[:, SUM, k : k + 1],
            )
            if k == 0:
                nc.scalar.activation(out=neg_guess[:], in_=sums[:, SUM, 0:1], func=FUNC.Copy, scale=-1.0 / BANK)
            if k == 3:
                row_factors(x_side, M_TILES - 1)
                normalise_x(M_TILES - 1)
            product_h(1, k)
            if k == 0:
                mean_and_var(x_side, M_TILES - 1)
        square_and_sum(1)
        mean_and_var(h_side, 1)
        for m in range(1, M_TILES - 1):
            row_factors_h(m)
            for k in range(CHUNKS):
                take_out_h(m, k, V if k in ON_VECTOR[m] else S)
            for k in range(CHUNKS):
                product_h(m + 1, k)
            mean_and_var(h_side, m + 1)
            square_and_sum((0, 5, 0)[m])
            if m == 1:
                normalise_from_sums(h_side, 0)
            for engine in GATES_ON[m]:
                if len(turned_gates) == 0:
                    turn_next_gate()
                    turn_next_gate()
                start_next_gate(engine)
            while len(turned_gates) < 2:
                turn_next_gate()
        m = M_TILES - 1
        row_factors_h(m)
        for k in range(CHUNKS):
            take_out_h(m, k, V if k in ON_VECTOR[m] else S)
        load_table_of(FUNC.Sigmoid)

        def turn_h_gate(gate, j, turned):
            live["h", gate, j] = turn(h_side, gate, j, turned)

        ALL = slice(0, BATCH)
        HALVES = (slice(0, BATCH // 2), slice(BATCH // 2, BATCH))

        def start_candidate(j):
            t = CAND * J_TILES + j
            cand = work.tile([P, BATCH], F32, name="cand", bufs=4)
            scale_and_shift(S, cand[:], live["h", CAND, j][:], column(gamma_u, t), column(beta_u, t))
            live[CAND, j] = cand

        def add_h_gate(gate, j):
            value = live[gate, j]
            nc.vector.scalar_tensor_tensor(
                out=value[:], in0=live["h", gate, j][:], scalar=column(gamma_u, gate * J_TILES + j), in1=value[:],
                op0=ALU.mult, op1=ALU.add,
            )

        def sigmoid_gate(gate, j):
            nc.scalar.activation(out=live[gate, j][:], in_=live[gate, j][:], func=FUNC.Sigmoid)

        def apply_reset(engine, j, part):
            cand = live[CAND, j][:, part]
            engine.tensor_tensor(out=cand, in0=cand, in1=live[RESET, j][:, part], op=ALU.mult)

        def add_x_candidate(j, part):
            cand = live[CAND, j][:, part]
            nc.vector.scalar_tensor_tensor(
                out=cand, in0=live["x", CAND, j][:, part], scalar=column(gamma_w, CAND * J_TILES + j), in1=cand,
                op0=ALU.mult, op1=ALU.add,
            )

        def finish_candidate(j, part):
            cand = live[CAND, j][:, part]
            nc.scalar.activation(out=cand, in_=cand, func=FUNC.Tanh, bias=column(shift, CAND * J_TILES + j))

        out_tiles = out.rearrange("(m p) n -> p m n", p=P)

        def turn_hx(j, turned):
            for m in range(M_TILES):
                nc.tensor.transpose(
                    out=turned[:, m * P : (m + 1) * P],
                    in_=h_side["x_sb"][:, m, j * P : (j + 1) * P],
                    identity=identity_bf16[:],
                )
            live["hx", j] = turned
            live["diff", j] = work.tile([P, BATCH], F32, name="diff")

        def blend_subtract(j, part):
            nc.vector.tensor_sub(
                out=live["diff", j][:, part], in0=live["hx", j][:, part], in1=live[CAND, j][:, part]
            )

        def blend_scale(engine, j, part):
            diff = live["diff", j][:, part]
            engine.tensor_tensor(out=diff, in0=diff, in1=live[UPDATE, j][:, part], op=ALU.mult)

        def turn_back(j, turned, part):
            for m in range(part.start // P, part.stop // P):
                batch = slice(m * P, (m + 1) * P)
                for name in (CAND, "diff"):
                    nc.tensor.matmul(
                        out=turned[:, batch], lhsT=live[name, j][:, batch], rhs=identity[:],
                        start=(name == CAND), stop=(name == "diff"), is_transpose=True,
                    )
            live["out", j] = turned

        def take_out_and_store(j, part):
            tiles = slice(part.start // P, part.stop // P)
            result = work.tile([P, M_TILES, P], F32, name="result")
            nc.scalar.copy(out=result[:, tiles, :], in_=live["out", j][:, part].rearrange("p (m n) -> p m n", n=P))
            nc.sync.dma_start(out=out_tiles[:, tiles, j * P : (j + 1) * P], in_=result[:, tiles, :])

        H_RESET, H_CAND, H_UPDATE, X_CAND, HX, BACK = 0, 1, 2, 3, 4, 5

        last = J_TILES - 1
        turn_h_gate(CAND, 0, bank(H_CAND))
        turn_h_gate(RESET, 0, bank(H_RESET))
        turn_h_gate(UPDATE, 0, bank(H_UPDATE))
        for j in range(last + 1):
            start_candidate(j)
            add_h_gate(RESET, j)
            sigmoid_gate(RESET, j)
            if j >= 1:
                turn_hx(j - 1, bank(HX, dtype=BF16))
            if j >= 1:
                turn_next_gate()
            if j < last:
                turn_h_gate(RESET, j + 1, bank(H_RESET))
                turn_h_gate(CAND, j + 1, bank(H_CAND))
                apply_reset(nc.gpsimd, j, ALL)
            if j >= 1:
                add_x_candidate(j - 1, ALL)
                finish_candidate(j - 1, ALL)
            turn_x_gate(CAND, j, bank(X_CAND))
            add_h_gate(UPDATE, j)
            sigmoid_gate(UPDATE, j)
            for _ in range(3 if j == 0 else 1):
                start_next_gate(V)
            if 1 <= j < last:
                blend_subtract(j - 1, ALL)
                blend_scale(nc.gpsimd, j - 1, ALL)
            if j >= 2:
                turn_back(j - 2, bank(BACK), ALL)
            if j < last:
                turn_h_gate(UPDATE, j + 1, bank(H_UPDATE))
            if j >= 2:
                take_out_and_store(j - 2, ALL)
        back = (bank(H_RESET), bank(H_UPDATE))
        for part in HALVES:
            apply_reset(nc.vector, last, part)
            add_x_candidate(last, part)
            finish_candidate(last, part)
        blend_subtract(last - 1, ALL)
        blend_scale(nc.vector, last - 1, ALL)
        turn_hx(last, bank(HX, dtype=BF16))
        turn_back(last - 1, bank(BACK), ALL)
        take_out_and_store(last - 1, ALL)
        for part in HALVES:
            blend_subtract(last, part)
            blend_scale(nc.vector, last, part)
        for part, turned in zip(HALVES, back):
            turn_back(last, turned, part)
            take_out_and_store(last, part)
